import numpy as np
import ml_dtypes


def mxq(x, axis, fmt="e4m3"):
    dtype, down = {"e4m3": (ml_dtypes.float8_e4m3fn, 7), "e5m2": (ml_dtypes.float8_e5m2, 14)}[fmt]
    v = np.moveaxis(np.asarray(x, np.float32).astype(ml_dtypes.bfloat16).astype(np.float64), axis, -1)
    blocks = v.reshape(v.shape[:-1] + (-1, 32))
    amax = np.abs(blocks).max(-1, keepdims=True)
    byte = np.maximum(np.where(amax > 0, np.frexp(amax)[1] - 1 + 127, 0) - down, 1)
    scale = np.exp2(byte - 127.0)
    codes = (blocks / scale).astype(np.float32).astype(dtype).astype(np.float64)
    return np.moveaxis((codes * scale).reshape(v.shape), -1, axis)


WIDE = False


def mx_kscale(k):
    if not WIDE:
        return np.ones(k)
    levels = np.array([10, -10, 5, -5, 0])
    if k % 512:
        return np.exp2(np.random.permutation(np.resize(levels, k // 32))).repeat(32)
    a = np.empty((k // 512, 16))
    for p in range(k // 512):
        a[p, :8] = np.random.permutation(np.resize(levels, 8))
        for g in range(8):
            far = levels[np.abs(levels - a[p, g]) >= 10]
            a[p, g + 8] = far[np.random.randint(len(far))]
    return np.exp2(a.ravel()).repeat(32)


BF16 = ml_dtypes.bfloat16


def bf(x):
    return np.asarray(x, np.float32).astype(BF16)


def f64(x):
    return np.asarray(x).astype(np.float64)


B, L, D, H, QK, V = 4, 512, 1024, 8, 128, 128


def setup_inputs():
    s = mx_kscale(L)
    return {"q_rot": bf(np.random.standard_normal((H, B, L, QK)) * 0.3),
            "k_rot": bf(np.random.standard_normal((H, B, L, QK)) * 0.3 * s[:, None]),
            "v": bf(np.random.standard_normal((H, B, L, V)) * 0.5 / s[:, None]),
            "times": bf(np.broadcast_to(np.arange(L), (B, L)))}


def reference(q_rot, k_rot, v, times):
    gammas = 1.0 - 2.0 ** (-5.0 - np.arange(H))
    t = f64(times)
    mat = t[:, :, None] - t[:, None, :]
    mask = mat >= 0
    g4 = gammas[:, None, None, None]
    d = np.where(mask, g4 ** np.where(mask, mat, 0.0), 0.0)
    ret = (f64(q_rot) @ f64(k_rot).transpose(0, 1, 3, 2)) * d
    return mxq(ret, 3, "e4m3") @ mxq(f64(v), 2, "e4m3")

@@ -1,0 +1,211 @@
+import math
+from contextlib import ExitStack
+
+import concourse.mybir as mybir
+from concourse.masks import make_identity
+
+F32 = mybir.dt.float32
+BF16 = mybir.dt.bfloat16
+U32 = mybir.dt.uint32
+U8 = mybir.dt.uint8
+FP8X4 = mybir.dt.float8_e4m3fn_x4
+ALU = mybir.AluOpType
+ACT = mybir.ActivationFunctionType
+
+H, B, L, DH = 8, 4, 512, 128
+P = 128
+NT = L // P
+STEPS = H * B
+PAIR = 2
+FAR = 1.0e6
+LOG_GAMMA = [math.log(1.0 - 2.0 ** (-5 - h)) for h in range(H)]
+
+FLOPS = 2 * (2 * H * B * L * L * DH)
+
+
+def tile_multiscaleretention_pb_kernel(tc, q_rot, k_rot, v, times, out):
+    nc = tc.nc
+    q_rows = q_rot.flatten_outer_dims().rearrange("(g p) d -> p g d", p=P)
+    k_rows = k_rot.flatten_outer_dims().rearrange("(n p t) d -> p n t d", p=P, t=NT)
+    v_rows = v.flatten_outer_dims().rearrange("(n p t) d -> p n t d", p=P, t=NT)
+    out_rows = out.flatten_outer_dims().rearrange("(g p) d -> p g d", p=P)
+
+    with ExitStack() as stack:
+        stack.enter_context(tc.manual_schedule())
+        const = stack.enter_context(tc.tile_pool(name="const", bufs=1))
+        small = stack.enter_context(tc.tile_pool(name="small", bufs=2))
+        loads = stack.enter_context(tc.tile_pool(name="loads", bufs=3))
+        turned = stack.enter_context(tc.tile_pool(name="turned", bufs=3))
+        weighed = stack.enter_context(tc.tile_pool(name="weighed", bufs=2))
+        values = stack.enter_context(tc.tile_pool(name="values", bufs=3))
+        results = stack.enter_context(tc.tile_pool(name="results", bufs=3))
+        turn_psum = stack.enter_context(tc.psum_pool(name="turn_psum", bufs=2))
+        score_psum = stack.enter_context(tc.psum_pool(name="score_psum", bufs=NT))
+        out_psum = stack.enter_context(tc.psum_pool(name="out_psum", bufs=2))
+
+        q_sb, k_sb, v_sb = {}, {}, {}
+        v_codes, v_scales, v_grouped = {}, {}, {}
+        qk_t, scores, ret_bf, ret_codes, ret_scales = {}, {}, {}, {}, {}
+
+        def load(c):
+            slots = slice(c * PAIR * NT, (c + 1) * PAIR * NT)
+            steps = slice(c * PAIR, (c + 1) * PAIR)
+            q_sb[c] = loads.tile([P, PAIR * NT, DH], BF16, name="q_sb")
+            k_sb[c] = loads.tile([P, PAIR, NT, DH], BF16, name="k_sb")
+            v_sb[c] = loads.tile([P, PAIR, NT, DH], BF16, name="v_sb")
+            nc.sync.dma_start(out=q_sb[c][:], in_=q_rows[:, slots, :])
+            nc.sync.dma_start(out=k_sb[c][:], in_=k_rows[:, steps, :, :])
+            nc.sync.dma_start(out=v_sb[c][:], in_=v_rows[:, steps, :, :])
+
+        def regroup_v(c):
+            v_grouped[c] = values.tile([P, PAIR, DH, NT], BF16, name="v_grouped", align_bytes=64)
+            nc.scalar.copy(out=v_grouped[c][:], in_=v_sb[c][:].rearrange("p b t d -> p b d t"))
+
+        def quantise_v(c):
+            v_codes[c] = values.tile([P, PAIR, DH], U32, name="v_codes", align_bytes=64)
+            v_scales[c] = values.tile([P, PAIR, DH], U8, name="v_scales", align_bytes=64)
+            nc.vector.quantize_mx(
+                out=v_codes[c][:].rearrange("p b d -> p (b d)").bitcast(FP8X4),
+                scales=v_scales[c][:].rearrange("p b d -> p (b d)"),
+                in_=v_grouped[c][:].rearrange("p b d t -> p (b d t)"),
+            )
+
+        def turn(n):
+            c, first = n // PAIR, (n % PAIR) * NT
+            bank = turn_psum.tile([P, 2 * NT, P], BF16, name="turn_bank")
+            for a in range(NT):
+                nc.tensor.transpose(out=bank[:, a, :], in_=q_sb[c][:, first + a, :], identity=ident[:])
+            for a in range(NT):
+                nc.tensor.transpose(
+                    out=bank[:, NT + a, :], in_=k_sb[c][:, n % PAIR, a, :], identity=ident[:]
+                )
+            qk_t[n] = turned.tile([P, 2 * NT, P], BF16, name="qk_t")
+            nc.scalar.copy(out=qk_t[n][:], in_=bank[:])
+
+        def decay_of(n):
+            h, b = divmod(n, B)
+            for i_tile in range(NT):
+                nc.scalar.activation(
+                    out=decay[b][:, i_tile, :, :],
+                    in_=delta[b][:, i_tile, :, :],
+                    func=ACT.Exp,
+                    scale=LOG_GAMMA[h],
+                )
+
+        def score(n, i_tile):
+            scores[n, i_tile] = score_psum.tile([P, NT, P], F32, name="score_bank")
+            for t in range(NT):
+                nc.tensor.matmul(
+                    out=scores[n, i_tile][:, t, :],
+                    lhsT=qk_t[n][:, NT + t, :],
+                    rhs=qk_t[n][:, i_tile, :],
+                    start=True,
+                    stop=True,
+                )
+
+        def weigh(n, i_tile):
+            b = n % B
+            if i_tile == 0:
+                ret_bf[n] = weighed.tile([P, NT, P, NT], BF16, name="ret_bf", align_bytes=64)
+            nc.vector.tensor_tensor(
+                out=ret_bf[n][:, i_tile, :, :],
+                in0=scores[n, i_tile][:].rearrange("p t i -> p i t"),
+                in1=decay[b][:, i_tile, :, :].rearrange("p t i -> p i t"),
+                op=ALU.mult,
+            )
+
+        def quantise(n):
+            ret_codes[n] = weighed.tile([P, L], U32, name="ret_codes", align_bytes=64)
+            ret_scales[n] = weighed.tile([P, L], U8, name="ret_scales", align_bytes=64)
+            nc.vector.quantize_mx(
+                out=ret_codes[n][:].bitcast(FP8X4),
+                scales=ret_scales[n][:],
+                in_=ret_bf[n][:].rearrange("p a i t -> p (a i t)"),
+            )
+
+        def product(n):
+            c, half = n // PAIR, n % PAIR
+            bank = out_psum.tile([P, NT, DH], F32, name="out_bank")
+            for i_tile in range(NT):
+                cols = slice(i_tile * P, (i_tile + 1) * P)
+                nc.tensor.matmul_mx(
+                    out=bank[:, i_tile, :],
+                    lhsT=ret_codes[n][:, cols].bitcast(FP8X4),
+                    lhsT_scale=ret_scales[n][:, cols],
+                    rhs=v_codes[c][:, half, :].bitcast(FP8X4),
+                    rhs_scale=v_scales[c][:, half, :],
+                    start=True,
+                    stop=True,
+                )
+            out_sb = results.tile([P, NT, DH], F32, name="out_sb")
+            nc.scalar.copy(out=out_sb[:], in_=bank[:])
+            nc.sync.dma_start(out=out_rows[:, n * NT : (n + 1) * NT, :], in_=out_sb[:])
+
+        t_row = const.tile([P, B * L], BF16, name="t_row")
+        nc.scalar.dma_start(out=t_row[:], in_=times.rearrange("b l -> (b l)").partition_broadcast(P))
+        load(0)
+        load(1)
+        ident = const.tile([P, P], BF16, name="ident")
+        make_identity(nc, ident[:])
+
+        t_bank = out_psum.tile([P, NT, DH], F32, name="out_bank")
+        t_key = const.tile([P, B * NT], F32, name="t_key")
+        t_groups = t_row[:].rearrange("p (b g t) -> p b t g", b=B, t=NT)
+        for b in range(B):
+            for t in range(NT):
+                nc.tensor.matmul(
+                    out=t_bank[:, 0, b * NT + t : b * NT + t + 1],
+                    lhsT=t_groups[:, b, t, :],
+                    rhs=ident[:, 0:1],
+                    start=True,
+                    stop=True,
+                )
+        nc.vector.tensor_copy(out=t_key[:], in_=t_bank[:, 0, 0 : B * NT])
+
+        delta = [const.tile([P, NT, NT, P], F32, name="delta%d" % b) for b in range(B)]
+        decay = [const.tile([P, NT, NT, P], F32, name="decay%d" % b) for b in range(B)]
+
+        def prepare_times(b):
+            row = t_row[:, b * L : (b + 1) * L].rearrange("p (a i) -> p a i", i=P)
+            for t in range(NT):
+                key_time = t_key[:, b * NT + t : b * NT + t + 1]
+                dead = small.tile([P, NT, P], F32, name="dead")
+                nc.vector.tensor_scalar(
+                    out=dead[:], in0=row, scalar1=key_time, scalar2=FAR,
+                    op0=ALU.is_lt, op1=ALU.mult,
+                )
+                nc.vector.scalar_tensor_tensor(
+                    out=delta[b][:, :, t, :], in0=row, scalar=key_time, in1=dead[:],
+                    op0=ALU.subtract, op1=ALU.max,
+                )
+
+        turn(0)
+        prepare_times(0)
+        decay_of(0)
+        for i_tile in range(NT):
+            score(0, i_tile)
+        turn(1)
+        prepare_times(1)
+        decay_of(1)
+        regroup_v(0)
+        prepare_times(2)
+        prepare_times(3)
+        quantise_v(0)
+        for s in range(STEPS + 1):
+            if s % PAIR == 0 and s // PAIR + 2 < STEPS // PAIR:
+                load(s // PAIR + 2)
+            if s + 2 < STEPS:
+                decay_of(s + 2)
+                turn(s + 2)
+            for i_tile in range(NT):
+                if s < STEPS:
+                    weigh(s, i_tile)
+                if s + 1 < STEPS:
+                    score(s + 1, i_tile)
+                if i_tile == 0 and s >= 1:
+                    quantise(s - 1)
+                    product(s - 1)
+            if s % PAIR == 0 and s // PAIR + 1 < STEPS // PAIR:
+                regroup_v(s // PAIR + 1)
+            if s % PAIR == 1 and s // PAIR + 1 < STEPS // PAIR:
+                quantise_v(s // PAIR + 1)

@@ -7,6 +7,7 @@ from concourse.masks import make_identity
 F32 = mybir.dt.float32
 BF16 = mybir.dt.bfloat16
 U32 = mybir.dt.uint32
+I32 = mybir.dt.int32
 U8 = mybir.dt.uint8
 FP8X4 = mybir.dt.float8_e4m3fn_x4
 ALU = mybir.AluOpType
@@ -14,10 +15,31 @@ ACT = mybir.ActivationFunctionType
 
 H, B, L, DH = 8, 4, 512, 128
 P = 128
-NT = L // P
-STEPS = H * B
-PAIR = 2
-FAR = 1.0e6
+T = 4
+QP = 32
+QUARTERS = 4
+PAIRS = H * B // 2
+SETS = B // 2
+HEADS = 2
+TAIL = 32
+GAP = P - QP
+STRIDE = P + GAP
+UNITS = 6
+UNIT_COLS = [P, P, P, P, P, 2 * TAIL]
+UNIT_AT = [0, P, 2 * P, 3 * P, 4 * P, 5 * P]
+COLS = 5 * P + 2 * TAIL
+SLOT_G1, SLOT_G2, SLOT_G3, SLOT_G0 = 0, 1, 2, 3
+UNIT_PARTS = [
+    ((1, SLOT_G1), (1, SLOT_G1)),
+    ((2, SLOT_G2), (0, SLOT_G0)),
+    ((0, SLOT_G0), (2, SLOT_G2)),
+    ((3, SLOT_G3), None),
+    (None, (3, SLOT_G3)),
+]
+V_BYTES = HEADS * DH * 5
+V_CODES = HEADS * DH * 4
+NEVER = -(2.0**16)
+STEEP = 2.0**40
 LOG_GAMMA = [math.log(1.0 - 2.0 ** (-5 - h)) for h in range(H)]
 
 FLOPS = 2 * (2 * H * B * L * L * DH)
@@ -25,187 +47,402 @@ FLOPS = 2 * (2 * H * B * L * L * DH)
 
 def tile_multiscaleretention_pb_kernel(tc, q_rot, k_rot, v, times, out):
     nc = tc.nc
-    q_rows = q_rot.flatten_outer_dims().rearrange("(g p) d -> p g d", p=P)
-    k_rows = k_rot.flatten_outer_dims().rearrange("(n p t) d -> p n t d", p=P, t=NT)
-    v_rows = v.flatten_outer_dims().rearrange("(n p t) d -> p n t d", p=P, t=NT)
-    out_rows = out.flatten_outer_dims().rearrange("(g p) d -> p g d", p=P)
 
     with ExitStack() as stack:
         stack.enter_context(tc.manual_schedule())
         const = stack.enter_context(tc.tile_pool(name="const", bufs=1))
-        small = stack.enter_context(tc.tile_pool(name="small", bufs=2))
-        loads = stack.enter_context(tc.tile_pool(name="loads", bufs=3))
+        loads = stack.enter_context(tc.tile_pool(name="loads", bufs=4))
         turned = stack.enter_context(tc.tile_pool(name="turned", bufs=3))
+        decays = stack.enter_context(tc.tile_pool(name="decays", bufs=3))
         weighed = stack.enter_context(tc.tile_pool(name="weighed", bufs=2))
-        values = stack.enter_context(tc.tile_pool(name="values", bufs=3))
+        values = stack.enter_context(tc.tile_pool(name="values", bufs=2))
         results = stack.enter_context(tc.tile_pool(name="results", bufs=3))
-        turn_psum = stack.enter_context(tc.psum_pool(name="turn_psum", bufs=2))
-        score_psum = stack.enter_context(tc.psum_pool(name="score_psum", bufs=NT))
-        out_psum = stack.enter_context(tc.psum_pool(name="out_psum", bufs=2))
+        turn_psum = stack.enter_context(tc.psum_pool(name="turn_psum", bufs=1))
+        score_psum = stack.enter_context(tc.psum_pool(name="score_psum", bufs=4))
+        out_psum = stack.enter_context(tc.psum_pool(name="out_psum", bufs=1))
 
-        q_sb, k_sb, v_sb = {}, {}, {}
-        v_codes, v_scales, v_grouped = {}, {}, {}
-        qk_t, scores, ret_bf, ret_codes, ret_scales = {}, {}, {}, {}, {}
+        q_sb, k_sb, v_sb, v_grouped = {}, {}, {}, {}
+        q_t, scores, decay, ret_bf, ret_codes, ret_scales = {}, {}, {}, {}, {}, {}
 
-        def load(c):
-            slots = slice(c * PAIR * NT, (c + 1) * PAIR * NT)
-            steps = slice(c * PAIR, (c + 1) * PAIR)
-            q_sb[c] = loads.tile([P, PAIR * NT, DH], BF16, name="q_sb")
-            k_sb[c] = loads.tile([P, PAIR, NT, DH], BF16, name="k_sb")
-            v_sb[c] = loads.tile([P, PAIR, NT, DH], BF16, name="v_sb")
-            nc.sync.dma_start(out=q_sb[c][:], in_=q_rows[:, slots, :])
-            nc.sync.dma_start(out=k_sb[c][:], in_=k_rows[:, steps, :, :])
-            nc.sync.dma_start(out=v_sb[c][:], in_=v_rows[:, steps, :, :])
+        def head_of(s):
+            return s % H
 
-        def regroup_v(c):
-            v_grouped[c] = values.tile([P, PAIR, DH, NT], BF16, name="v_grouped", align_bytes=64)
-            nc.scalar.copy(out=v_grouped[c][:], in_=v_sb[c][:].rearrange("p b t d -> p b d t"))
+        def first_b(s):
+            return 2 * (s // H)
 
-        def quantise_v(c):
-            v_codes[c] = values.tile([P, PAIR, DH], U32, name="v_codes", align_bytes=64)
-            v_scales[c] = values.tile([P, PAIR, DH], U8, name="v_scales", align_bytes=64)
-            nc.vector.quantize_mx(
-                out=v_codes[c][:].rearrange("p b d -> p (b d)").bitcast(FP8X4),
-                scales=v_scales[c][:].rearrange("p b d -> p (b d)"),
-                in_=v_grouped[c][:].rearrange("p b d t -> p (b d t)"),
+        ident = const.tile([P, P], BF16, name="ident")
+        swapped = const.tile([P, P], BF16, name="swapped")
+        t_row = const.tile([P, TAIL + L], BF16, name="t_row")
+        key_row = const.tile([P, 2 * T, STRIDE], BF16, name="key_row")
+        ones = [const.tile([P, GAP + P + GAP], BF16, name="ones%d" % b) for b in range(B)]
+        q_time = [const.tile([P, COLS], F32, name="q_time%d" % g) for g in range(SETS)]
+        k_time = [const.tile([P, 5 * T], F32, name="k_time%d" % g) for g in range(SETS)]
+        diff = const.tile([P, COLS, T], F32, name="diff")
+        delta = [const.tile([P, COLS, T], F32, name="delta%d" % g) for g in range(SETS)]
+        k_t = [const.tile([P, 2 * T, STRIDE], BF16, name="k_t%d" % r) for r in range(3)]
+        tail_codes = [const.tile([P, 2 * P], U32, name="tail_codes%d" % r, align_bytes=64) for r in range(2)]
+        tail_scales = [const.tile([P, 2 * P], U8, name="tail_scales%d" % r, align_bytes=64) for r in range(2)]
+        v_parts = [
+            [
+                [
+                    const.tile([P, V_BYTES], U8, name="v_part%d_%d_%d" % (r, w, a), align_bytes=64)
+                    for a in range(QUARTERS)
+                ]
+                for w in range(2)
+            ]
+            for r in range(3)
+        ]
+
+        def load_qk(s):
+            h, b0 = head_of(s), first_b(s)
+            k_sb[s] = loads.tile([P, 2, T * DH], BF16, name="k_sb")
+            q_sb[s] = loads.tile([P, 2, T * DH], BF16, name="q_sb")
+            nc.sync.dma_start(
+                out=k_sb[s][:], in_=k_rot[h, b0 : b0 + 2].rearrange("b (p t) d -> p b (t d)", t=T)
+            )
+            nc.sync.dma_start(
+                out=q_sb[s][:], in_=q_rot[h, b0 : b0 + 2].rearrange("b (p t) d -> p b (t d)", t=T)
             )
 
-        def turn(n):
-            c, first = n // PAIR, (n % PAIR) * NT
-            bank = turn_psum.tile([P, 2 * NT, P], BF16, name="turn_bank")
-            for a in range(NT):
-                nc.tensor.transpose(out=bank[:, a, :], in_=q_sb[c][:, first + a, :], identity=ident[:])
-            for a in range(NT):
-                nc.tensor.transpose(
-                    out=bank[:, NT + a, :], in_=k_sb[c][:, n % PAIR, a, :], identity=ident[:]
-                )
-            qk_t[n] = turned.tile([P, 2 * NT, P], BF16, name="qk_t")
-            nc.scalar.copy(out=qk_t[n][:], in_=bank[:])
+        def load_v(g, which):
+            h, b = head_of(g * HEADS), first_b(g * HEADS) + which
+            v_sb[g, which] = loads.tile([P, HEADS, T, DH], BF16, name="v_sb%d" % which)
+            flat = v_sb[g, which][:].rearrange("p h t d -> p h (t d)")
+            rows = v[h : h + HEADS, b].rearrange("h (p t) d -> p h (t d)", t=T)
+            if which == 1:
+                nc.sync.dma_start(out=flat, in_=rows)
+            else:
+                for c in range(QUARTERS):
+                    at = (QUARTERS - 1 - c) * QP
+                    nc.sync.dma_start(
+                        out=flat[at : at + QP], in_=rows[c * QP : (c + 1) * QP]
+                    )
 
-        def decay_of(n):
-            h, b = divmod(n, B)
-            for i_tile in range(NT):
-                nc.scalar.activation(
-                    out=decay[b][:, i_tile, :, :],
-                    in_=delta[b][:, i_tile, :, :],
-                    func=ACT.Exp,
-                    scale=LOG_GAMMA[h],
-                )
+        def regroup_v(g, which):
+            v_grouped[g, which] = values.tile([P, HEADS, DH, T], BF16, name="v_grouped", align_bytes=64)
+            nc.vector.tensor_copy(
+                out=v_grouped[g, which][:], in_=v_sb[g, which][:].rearrange("p h t d -> p h d t")
+            )
 
-        def score(n, i_tile):
-            scores[n, i_tile] = score_psum.tile([P, NT, P], F32, name="score_bank")
-            for t in range(NT):
-                nc.tensor.matmul(
-                    out=scores[n, i_tile][:, t, :],
-                    lhsT=qk_t[n][:, NT + t, :],
-                    rhs=qk_t[n][:, i_tile, :],
-                    start=True,
-                    stop=True,
-                )
+        def quantise_v(g, which):
+            parts = v_parts[g % 3][which]
+            full = parts[QUARTERS - 1]
+            nc.vector.quantize_mx(
+                out=full[:, 0:V_CODES].bitcast(FP8X4),
+                scales=full[:, V_CODES:V_BYTES],
+                in_=v_grouped[g, which][:].rearrange("p h d t -> p (h d t)"),
+            )
+            for a in range(QUARTERS - 1):
+                live = (a + 1) * QP
+                if which == 0:
+                    dst, src = slice(0, live), slice(P - live, P)
+                else:
+                    dst, src = slice(P - live, P), slice(0, live)
+                nc.sync.dma_start(out=parts[a][dst, :].bitcast(I32), in_=full[src, :].bitcast(I32))
 
-        def weigh(n, i_tile):
-            b = n % B
-            if i_tile == 0:
-                ret_bf[n] = weighed.tile([P, NT, P, NT], BF16, name="ret_bf", align_bytes=64)
+        def turn(s):
+            k_bank = turn_psum.tile([P, 2 * T, P], BF16, name="k_bank")
+            for w in range(2):
+                for t in range(T):
+                    nc.tensor.transpose(
+                        out=k_bank[:, w * T + t, :],
+                        in_=k_sb[s][:, w, t * DH : (t + 1) * DH],
+                        identity=swapped[:] if w == 0 else ident[:],
+                    )
+            q_bank = turn_psum.tile([P, 2 * T, P], BF16, name="q_bank")
+            for w in range(2):
+                for t in range(T):
+                    nc.tensor.transpose(
+                        out=q_bank[:, w * T + t, :],
+                        in_=q_sb[s][:, w, t * DH : (t + 1) * DH],
+                        identity=ident[:],
+                    )
+            nc.scalar.copy(out=k_t[s % 3][:, :, 0:P], in_=k_bank[:])
+            q_t[s] = turned.tile([P, 2, L], BF16, name="q_t")
+            grouped = q_bank[:].rearrange("d (w t) p -> d w p t", t=T)
+            cut = P - TAIL // T
+            nc.scalar.copy(
+                out=q_t[s][:, :, TAIL:L].rearrange("d w (p t) -> d w p t", t=T),
+                in_=grouped[:, :, 0:cut, :],
+            )
+            nc.scalar.copy(
+                out=q_t[s][:, :, 0:TAIL].rearrange("d w (p t) -> d w p t", t=T),
+                in_=grouped[:, :, cut:P, :],
+            )
+
+        def query_cols(slot):
+            return slice(0, P) if slot == SLOT_G0 else slice((slot + 1) * P, (slot + 2) * P)
+
+        def key_window(wide, w, t, a):
+            flat = wide[:].rearrange("p j c -> p (j c)")
+            at = (w * T + t) * STRIDE + (1 - 2 * w) * (QUARTERS - 1 - a) * QP
+            return flat[:, at : at + P]
+
+        def score(s, u):
+            bank = score_psum.tile([P, T, P], F32, name="score_bank")
+            scores[s, u] = bank
+            keys = k_t[s % 3]
+            for t in range(T):
+                if u < 5:
+                    parts = [(w, part) for w, part in enumerate(UNIT_PARTS[u]) if part is not None]
+                    for n, (w, (a, slot)) in enumerate(parts):
+                        nc.tensor.matmul(
+                            out=bank[:, t, :],
+                            lhsT=key_window(keys, w, t, a),
+                            rhs=q_t[s][:, w, query_cols(slot)],
+                            start=n == 0,
+                            stop=n == len(parts) - 1,
+                        )
+                else:
+                    for w in range(2):
+                        nc.tensor.matmul(
+                            out=bank[:, t, w * TAIL : (w + 1) * TAIL],
+                            lhsT=key_window(keys, w, t, QUARTERS - 1),
+                            rhs=q_t[s][:, w, 0:TAIL],
+                            start=True,
+                            stop=True,
+                        )
+
+        def decay_of(s, units):
+            if s not in decay:
+                decay[s] = decays.tile([P, COLS, T], F32, name="decay")
+            cols = slice(UNIT_AT[units[0]], UNIT_AT[units[-1]] + UNIT_COLS[units[-1]])
+            nc.scalar.activation(
+                out=decay[s][:, cols, :], in_=delta[s // H][:, cols, :], func=ACT.Exp,
+                scale=LOG_GAMMA[head_of(s)],
+            )
+
+        def weigh(s, u):
+            if u == 0:
+                ret_bf[s] = weighed.tile([P, COLS, T], BF16, name="ret_bf", align_bytes=64)
+            cols = slice(UNIT_AT[u], UNIT_AT[u] + UNIT_COLS[u])
             nc.vector.tensor_tensor(
-                out=ret_bf[n][:, i_tile, :, :],
-                in0=scores[n, i_tile][:].rearrange("p t i -> p i t"),
-                in1=decay[b][:, i_tile, :, :].rearrange("p t i -> p i t"),
+                out=ret_bf[s][:, cols, :],
+                in0=scores[s, u][:, :, 0 : UNIT_COLS[u]].rearrange("p t i -> p i t"),
+                in1=decay[s][:, cols, :],
                 op=ALU.mult,
             )
 
-        def quantise(n):
-            ret_codes[n] = weighed.tile([P, L], U32, name="ret_codes", align_bytes=64)
-            ret_scales[n] = weighed.tile([P, L], U8, name="ret_scales", align_bytes=64)
+        def quantise(s, at, width, codes, scales):
             nc.vector.quantize_mx(
-                out=ret_codes[n][:].bitcast(FP8X4),
-                scales=ret_scales[n][:],
-                in_=ret_bf[n][:].rearrange("p a i t -> p (a i t)"),
+                out=codes.bitcast(FP8X4),
+                scales=scales,
+                in_=ret_bf[s][:, at : at + width, :].rearrange("p i t -> p (i t)"),
             )
 
-        def product(n):
-            c, half = n // PAIR, n % PAIR
-            bank = out_psum.tile([P, NT, DH], F32, name="out_bank")
-            for i_tile in range(NT):
-                cols = slice(i_tile * P, (i_tile + 1) * P)
-                nc.tensor.matmul_mx(
-                    out=bank[:, i_tile, :],
-                    lhsT=ret_codes[n][:, cols].bitcast(FP8X4),
-                    lhsT_scale=ret_scales[n][:, cols],
-                    rhs=v_codes[c][:, half, :].bitcast(FP8X4),
-                    rhs_scale=v_scales[c][:, half, :],
-                    start=True,
-                    stop=True,
-                )
-            out_sb = results.tile([P, NT, DH], F32, name="out_sb")
-            nc.scalar.copy(out=out_sb[:], in_=bank[:])
-            nc.sync.dma_start(out=out_rows[:, n * NT : (n + 1) * NT, :], in_=out_sb[:])
+        def quantise_main(s):
+            ret_codes[s] = weighed.tile([P, 5 * P], U32, name="ret_codes", align_bytes=64)
+            ret_scales[s] = weighed.tile([P, 5 * P], U8, name="ret_scales", align_bytes=64)
+            quantise(s, 0, 4 * P, ret_codes[s][:, 0 : 4 * P], ret_scales[s][:, 0 : 4 * P])
 
-        t_row = const.tile([P, B * L], BF16, name="t_row")
-        nc.scalar.dma_start(out=t_row[:], in_=times.rearrange("b l -> (b l)").partition_broadcast(P))
-        load(0)
-        load(1)
-        ident = const.tile([P, P], BF16, name="ident")
+        def quantise_rest(s):
+            quantise(s, 4 * P, P, ret_codes[s][:, 4 * P : 5 * P], ret_scales[s][:, 4 * P : 5 * P])
+            for w in range(2):
+                cols = slice(w * P, w * P + TAIL)
+                quantise(s, 5 * P + w * TAIL, TAIL, tail_codes[s % 2][:, cols], tail_scales[s % 2][:, cols])
+
+        def product(s):
+            h, b0 = head_of(s), first_b(s)
+            e = s % HEADS
+            out_sb = results.tile([P, 2, 4, DH], F32, name="out_sb")
+            for w in range(2):
+                parts = v_parts[(s // HEADS) % 3][w]
+                bank = out_psum.tile([P, 4, DH], F32, name="out_bank%d" % w)
+
+                def multiply(slot, codes, scales, a, start, stop):
+                    nc.tensor.matmul_mx(
+                        out=bank[:, slot, :],
+                        lhsT=codes.bitcast(FP8X4),
+                        lhsT_scale=scales,
+                        rhs=parts[a][:, e * 4 * DH : (e + 1) * 4 * DH].bitcast(FP8X4),
+                        rhs_scale=parts[a][:, V_CODES + e * DH : V_CODES + (e + 1) * DH],
+                        start=start,
+                        stop=stop,
+                    )
+
+                for u in range(5):
+                    part = UNIT_PARTS[u][w]
+                    if part is None:
+                        continue
+                    a, slot = part
+                    cols = slice(u * P, (u + 1) * P)
+                    has_tail = slot == SLOT_G0
+                    multiply(slot, ret_codes[s][:, cols], ret_scales[s][:, cols], a, True, not has_tail)
+                    if has_tail:
+                        tail = slice(w * P, (w + 1) * P)
+                        multiply(
+                            slot, tail_codes[s % 2][:, tail], tail_scales[s % 2][:, tail],
+                            QUARTERS - 1, False, True,
+                        )
+                nc.scalar.copy(out=out_sb[:, w, :, :], in_=bank[:])
+                nc.sync.dma_start(
+                    out=out[h, b0 + w, P - TAIL : L - TAIL, :].rearrange("(a p) d -> p a d", p=P),
+                    in_=out_sb[:, w, 0:3, :],
+                )
+            nc.sync.dma_start(
+                out=out[h, b0 : b0 + 2, 0 : P - TAIL, :].rearrange("b p d -> p b d"),
+                in_=out_sb[TAIL:P, :, 3, :],
+            )
+            nc.sync.dma_start(
+                out=out[h, b0 : b0 + 2, L - TAIL : L, :].rearrange("b p d -> p b d"),
+                in_=out_sb[0:TAIL, :, 3, :],
+            )
+
+        nc.vector.memset(t_row[:].bitcast(U32), 0)
+        nc.sync.dma_start(out=t_row[0:P:32, TAIL : TAIL + L], in_=times)
+        load_qk(0)
+        load_qk(1)
+        load_v(0, 0)
+        load_v(0, 1)
+        load_qk(2)
+        load_v(1, 0)
+        load_v(1, 1)
+        nc.vector.memset(key_row[:].rearrange("p j c -> p (j c)").bitcast(U32), 0)
+        nc.vector.memset(t_row[:, 0:TAIL], NEVER)
         make_identity(nc, ident[:])
-
-        t_bank = out_psum.tile([P, NT, DH], F32, name="out_bank")
-        t_key = const.tile([P, B * NT], F32, name="t_key")
-        t_groups = t_row[:].rearrange("p (b g t) -> p b t g", b=B, t=NT)
         for b in range(B):
-            for t in range(NT):
+            nc.gpsimd.memset(ones[b][:].bitcast(U32), 0)
+            nc.gpsimd.memset(ones[b][32 * b : 32 * b + 1, GAP : GAP + P], 1.0)
+        for c in range(QUARTERS):
+            far = QUARTERS - 1 - c
+            nc.vector.tensor_copy(
+                out=swapped[:, c * QP : (c + 1) * QP], in_=ident[:, far * QP : (far + 1) * QP]
+            )
+        for r in range(3):
+            nc.gpsimd.memset(
+                k_t[r][:].rearrange("p j c -> p (j c)").bitcast(U32).rearrange("p (j c) -> p j c", j=2 * T)[
+                    :, :, P // 2 : STRIDE // 2
+                ],
+                0,
+            )
+
+        times_only = t_row[:, TAIL : TAIL + L]
+        for c in range(QUARTERS):
+            far = QUARTERS - 1 - c
+            nc.vector.tensor_copy(
+                out=key_row[:, 0:T, far * QP : (far + 1) * QP],
+                in_=times_only[:, c * P : (c + 1) * P].rearrange("p (r t) -> p t r", t=T),
+            )
+        nc.vector.tensor_copy(
+            out=key_row[:, T : 2 * T, 0:P], in_=times_only.rearrange("p (m t) -> p t m", t=T)
+        )
+
+        def ones_window(b, w, a):
+            at = GAP + (1 - 2 * w) * (QUARTERS - 1 - a) * QP
+            return ones[b][:, at : at + P]
+
+        def time_banks(g):
+            bank_a = out_psum.tile([P, T, P], F32, name="out_bank0")
+            bank_b = out_psum.tile([P, T, P], F32, name="out_bank1")
+            for u in range(5):
+                parts = [(w, part) for w, part in enumerate(UNIT_PARTS[u]) if part is not None]
+                dst = bank_a[:, u, :] if u < 4 else bank_b[:, 0, :]
+                for n, (w, (a, slot)) in enumerate(parts):
+                    nc.tensor.matmul(
+                        out=dst,
+                        lhsT=ones_window(2 * g + w, w, a),
+                        rhs=t_row[:, query_cols(slot)],
+                        start=n == 0,
+                        stop=n == len(parts) - 1,
+                    )
+                for t in range(T):
+                    for n, (w, (a, slot)) in enumerate(parts):
+                        b = 2 * g + w
+                        nc.tensor.matmul(
+                            out=bank_b[:, 2, u * T + t : u * T + t + 1],
+                            lhsT=key_window(key_row, w, t, a),
+                            rhs=ident[:, 32 * b : 32 * b + 1],
+                            start=n == 0,
+                            stop=n == len(parts) - 1,
+                        )
+            for w in range(2):
                 nc.tensor.matmul(
-                    out=t_bank[:, 0, b * NT + t : b * NT + t + 1],
-                    lhsT=t_groups[:, b, t, :],
-                    rhs=ident[:, 0:1],
+                    out=bank_b[:, 1, w * TAIL : (w + 1) * TAIL],
+                    lhsT=ones_window(2 * g + w, w, QUARTERS - 1),
+                    rhs=t_row[:, L : L + TAIL],
                     start=True,
                     stop=True,
                 )
-        nc.vector.tensor_copy(out=t_key[:], in_=t_bank[:, 0, 0 : B * NT])
+            nc.vector.tensor_copy(out=k_time[g][:], in_=bank_b[:, 2, 0 : 5 * T])
+            nc.vector.tensor_copy(
+                out=q_time[g][:, 0 : 4 * P], in_=bank_a[:].rearrange("p u i -> p (u i)")
+            )
+            nc.scalar.copy(
+                out=q_time[g][:, 4 * P : COLS],
+                in_=bank_b[:].rearrange("p u i -> p (u i)")[:, 0 : P + 2 * TAIL],
+            )
 
-        delta = [const.tile([P, NT, NT, P], F32, name="delta%d" % b) for b in range(B)]
-        decay = [const.tile([P, NT, NT, P], F32, name="decay%d" % b) for b in range(B)]
-
-        def prepare_times(b):
-            row = t_row[:, b * L : (b + 1) * L].rearrange("p (a i) -> p a i", i=P)
-            for t in range(NT):
-                key_time = t_key[:, b * NT + t : b * NT + t + 1]
-                dead = small.tile([P, NT, P], F32, name="dead")
-                nc.vector.tensor_scalar(
-                    out=dead[:], in0=row, scalar1=key_time, scalar2=FAR,
-                    op0=ALU.is_lt, op1=ALU.mult,
+        def subtract(g, u, engine):
+            at = UNIT_AT[u]
+            pieces = [(u, at, P)] if u < 5 else [(3, at, TAIL), (4, at + TAIL, TAIL)]
+            for k_unit, at, width in pieces:
+                engine.tensor_tensor(
+                    out=diff[:, at : at + width, :],
+                    in0=q_time[g][:, at : at + width].unsqueeze(2).to_broadcast([P, width, T]),
+                    in1=k_time[g][:, k_unit * T : (k_unit + 1) * T].unsqueeze(1).to_broadcast([P, width, T]),
+                    op=ALU.subtract,
                 )
-                nc.vector.scalar_tensor_tensor(
-                    out=delta[b][:, :, t, :], in0=row, scalar=key_time, in1=dead[:],
-                    op0=ALU.subtract, op1=ALU.max,
-                )
 
+        def make_delta(g, u):
+            cols = slice(UNIT_AT[u], UNIT_AT[u] + UNIT_COLS[u])
+            nc.vector.scalar_tensor_tensor(
+                out=delta[g][:, cols, :], in0=diff[:, cols, :], scalar=-STEEP, in1=diff[:, cols, :],
+                op0=ALU.mult, op1=ALU.max,
+            )
+
+        order = [(s, u) for s in range(PAIRS) for u in range(UNITS)]
+        time_banks(0)
         turn(0)
-        prepare_times(0)
-        decay_of(0)
-        for i_tile in range(NT):
-            score(0, i_tile)
+        for u in range(UNITS):
+            subtract(0, u, nc.vector if u < 3 else nc.gpsimd)
+            make_delta(0, u)
+            decay_of(0, [u])
+            if u < 4:
+                score(*order[u])
         turn(1)
-        prepare_times(1)
-        decay_of(1)
-        regroup_v(0)
-        prepare_times(2)
-        prepare_times(3)
-        quantise_v(0)
-        for s in range(STEPS + 1):
-            if s % PAIR == 0 and s // PAIR + 2 < STEPS // PAIR:
-                load(s // PAIR + 2)
-            if s + 2 < STEPS:
-                decay_of(s + 2)
+        decay_of(1, [0, 1, 2])
+        decay_of(1, [3, 4, 5])
+        for r in range(3):
+            for w in range(2):
+                for a in range(QUARTERS):
+                    nc.gpsimd.memset(v_parts[r][w][a][:].bitcast(I32), 0)
+            if r < 2:
+                nc.gpsimd.memset(tail_codes[r][:], 0)
+                nc.gpsimd.memset(tail_scales[r][:].bitcast(I32), 0)
+        regroup_v(0, 0)
+        regroup_v(0, 1)
+        quantise_v(0, 0)
+        quantise_v(0, 1)
+        done = 4
+        for s in range(PAIRS + 1):
+            if s + 3 < PAIRS:
+                load_qk(s + 3)
+            g = s // HEADS + 2
+            if g * HEADS < PAIRS:
+                load_v(g, s % HEADS)
+            if s + 2 < PAIRS:
                 turn(s + 2)
-            for i_tile in range(NT):
-                if s < STEPS:
-                    weigh(s, i_tile)
-                if s + 1 < STEPS:
-                    score(s + 1, i_tile)
-                if i_tile == 0 and s >= 1:
-                    quantise(s - 1)
+            for u in range(UNITS):
+                if s < PAIRS:
+                    weigh(s, u)
+                    if done < len(order):
+                        score(*order[done])
+                        done += 1
+                if s + 2 < PAIRS and u % 2 == 0:
+                    decay_of(s + 2, [u, u + 1])
+                if u == 1 and s == 0:
+                    time_banks(1)
+                if u == 0 and s >= 1:
+                    quantise_main(s - 1)
+                if u == 1 and s >= 1:
+                    quantise_rest(s - 1)
                     product(s - 1)
-            if s % PAIR == 0 and s // PAIR + 1 < STEPS // PAIR:
-                regroup_v(s // PAIR + 1)
-            if s % PAIR == 1 and s // PAIR + 1 < STEPS // PAIR:
-                quantise_v(s // PAIR + 1)
+                g = s // HEADS + 1
+                if g * HEADS < PAIRS:
+                    if u == 3:
+                        regroup_v(g, s % HEADS)
+                    if u == 5:
+                        quantise_v(g, s % HEADS)
+            if s < UNITS:
+                subtract(1, s, nc.gpsimd)
+                make_delta(1, s)

@@ -120,9 +120,12 @@ def tile_multiscaleretention_pb_kernel(tc, q_rot, k_rot, v, times, out):
 
         def regroup_v(g, which):
             v_grouped[g, which] = values.tile([P, HEADS, DH, T], BF16, name="v_grouped", align_bytes=64)
-            nc.vector.tensor_copy(
-                out=v_grouped[g, which][:], in_=v_sb[g, which][:].rearrange("p h t d -> p h d t")
-            )
+            for e in range(HEADS):
+                nc.gpsimd.tensor_scalar(
+                    out=v_grouped[g, which][:, e],
+                    in0=v_sb[g, which][:, e].rearrange("p t d -> p d t"),
+                    scalar1=1.0, scalar2=0.0, op0=ALU.mult, op1=ALU.add,
+                )
 
         def quantise_v(g, which):
             parts = v_parts[g % 3][which]

@@ -120,6 +120,11 @@ def tile_multiscaleretention_pb_kernel(tc, q_rot, k_rot, v, times, out):
 
         def regroup_v(g, which):
             v_grouped[g, which] = values.tile([P, HEADS, DH, T], BF16, name="v_grouped", align_bytes=64)
+            if g == 0:
+                nc.vector.tensor_copy(
+                    out=v_grouped[g, which][:], in_=v_sb[g, which][:].rearrange("p h t d -> p h d t")
+                )
+                return
             for e in range(HEADS):
                 nc.gpsimd.tensor_scalar(
                     out=v_grouped[g, which][:, e],

@@ -52,7 +52,6 @@ def tile_multiscaleretention_pb_kernel(tc, q_rot, k_rot, v, times, out):
         stack.enter_context(tc.manual_schedule())
         const = stack.enter_context(tc.tile_pool(name="const", bufs=1))
         loads = stack.enter_context(tc.tile_pool(name="loads", bufs=4))
-        turned = stack.enter_context(tc.tile_pool(name="turned", bufs=3))
         decays = stack.enter_context(tc.tile_pool(name="decays", bufs=3))
         weighed = stack.enter_context(tc.tile_pool(name="weighed", bufs=2))
         values = stack.enter_context(tc.tile_pool(name="values", bufs=2))
@@ -62,7 +61,7 @@ def tile_multiscaleretention_pb_kernel(tc, q_rot, k_rot, v, times, out):
         out_psum = stack.enter_context(tc.psum_pool(name="out_psum", bufs=1))
 
         q_sb, k_sb, v_sb, v_grouped = {}, {}, {}, {}
-        q_t, scores, decay, ret_bf, ret_codes, ret_scales = {}, {}, {}, {}, {}, {}
+        scores, decay, ret_bf, ret_codes, ret_scales = {}, {}, {}, {}, {}
 
         def head_of(s):
             return s % H
@@ -80,6 +79,7 @@ def tile_multiscaleretention_pb_kernel(tc, q_rot, k_rot, v, times, out):
         diff = const.tile([P, COLS, T], F32, name="diff")
         delta = [const.tile([P, COLS, T], F32, name="delta%d" % g) for g in range(SETS)]
         k_t = [const.tile([P, 2 * T, STRIDE], BF16, name="k_t%d" % r) for r in range(3)]
+        q_t = [const.tile([P, 2, TAIL + L], BF16, name="q_t%d" % r) for r in range(3)]
         tail_codes = [const.tile([P, 2 * P], U32, name="tail_codes%d" % r, align_bytes=64) for r in range(2)]
         tail_scales = [const.tile([P, 2 * P], U8, name="tail_scales%d" % r, align_bytes=64) for r in range(2)]
         v_parts = [
@@ -96,12 +96,12 @@ def tile_multiscaleretention_pb_kernel(tc, q_rot, k_rot, v, times, out):
         def load_qk(s):
             h, b0 = head_of(s), first_b(s)
             k_sb[s] = loads.tile([P, 2, T * DH], BF16, name="k_sb")
-            q_sb[s] = loads.tile([P, 2, T * DH], BF16, name="q_sb")
+            q_sb[s] = loads.tile([P, 2 * T, DH], BF16, name="q_sb")
             nc.sync.dma_start(
                 out=k_sb[s][:], in_=k_rot[h, b0 : b0 + 2].rearrange("b (p t) d -> p b (t d)", t=T)
             )
             nc.sync.dma_start(
-                out=q_sb[s][:], in_=q_rot[h, b0 : b0 + 2].rearrange("b (p t) d -> p b (t d)", t=T)
+                out=q_sb[s][:], in_=q_rot[h, b0 : b0 + 2].rearrange("b l d -> (b l) d").rearrange("(a p) d -> p a d", p=P)
             )
 
         def load_v(g, which):
@@ -158,24 +158,12 @@ def tile_multiscaleretention_pb_kernel(tc, q_rot, k_rot, v, times, out):
                         identity=swapped[:] if w == 0 else ident[:],
                     )
             q_bank = turn_psum.tile([P, 2 * T, P], BF16, name="q_bank")
-            for w in range(2):
-                for t in range(T):
-                    nc.tensor.transpose(
-                        out=q_bank[:, w * T + t, :],
-                        in_=q_sb[s][:, w, t * DH : (t + 1) * DH],
-                        identity=ident[:],
-                    )
+            for a in range(2 * T):
+                nc.tensor.transpose(out=q_bank[:, a, :], in_=q_sb[s][:, a, :], identity=ident[:])
             nc.scalar.copy(out=k_t[s % 3][:, :, 0:P], in_=k_bank[:])
-            q_t[s] = turned.tile([P, 2, L], BF16, name="q_t")
-            grouped = q_bank[:].rearrange("d (w t) p -> d w p t", t=T)
-            cut = P - TAIL // T
             nc.scalar.copy(
-                out=q_t[s][:, :, TAIL:L].rearrange("d w (p t) -> d w p t", t=T),
-                in_=grouped[:, :, 0:cut, :],
-            )
-            nc.scalar.copy(
-                out=q_t[s][:, :, 0:TAIL].rearrange("d w (p t) -> d w p t", t=T),
-                in_=grouped[:, :, cut:P, :],
+                out=q_t[s % 3][:, :, TAIL : TAIL + L],
+                in_=q_bank[:].rearrange("d (w a) p -> d w (a p)", w=2),
             )
 
         def query_cols(slot):
@@ -197,7 +185,7 @@ def tile_multiscaleretention_pb_kernel(tc, q_rot, k_rot, v, times, out):
                         nc.tensor.matmul(
                             out=bank[:, t, :],
                             lhsT=key_window(keys, w, t, a),
-                            rhs=q_t[s][:, w, query_cols(slot)],
+                            rhs=q_t[s % 3][:, w, query_cols(slot)],
                             start=n == 0,
                             stop=n == len(parts) - 1,
                         )
@@ -206,7 +194,7 @@ def tile_multiscaleretention_pb_kernel(tc, q_rot, k_rot, v, times, out):
                         nc.tensor.matmul(
                             out=bank[:, t, w * TAIL : (w + 1) * TAIL],
                             lhsT=key_window(keys, w, t, QUARTERS - 1),
-                            rhs=q_t[s][:, w, 0:TAIL],
+                            rhs=q_t[s % 3][:, w, L : L + TAIL],
                             start=True,
                             stop=True,
                         )
@@ -323,6 +311,10 @@ def tile_multiscaleretention_pb_kernel(tc, q_rot, k_rot, v, times, out):
                 ],
                 0,
             )
+
+        for r in range(3):
+            for w in range(2):
+                nc.gpsimd.memset(q_t[r][:, w, 0:TAIL].bitcast(U32), 0)
 
         times_only = t_row[:, TAIL : TAIL + L]
         for c in range(QUARTERS):

@@ -51,7 +51,7 @@ def tile_multiscaleretention_pb_kernel(tc, q_rot, k_rot, v, times, out):
     with ExitStack() as stack:
         stack.enter_context(tc.manual_schedule())
         const = stack.enter_context(tc.tile_pool(name="const", bufs=1))
-        loads = stack.enter_context(tc.tile_pool(name="loads", bufs=4))
+        loads = stack.enter_context(tc.tile_pool(name="loads", bufs=6))
         decays = stack.enter_context(tc.tile_pool(name="decays", bufs=3))
         weighed = stack.enter_context(tc.tile_pool(name="weighed", bufs=2))
         values = stack.enter_context(tc.tile_pool(name="values", bufs=2))
@@ -293,6 +293,8 @@ def tile_multiscaleretention_pb_kernel(tc, q_rot, k_rot, v, times, out):
         load_qk(2)
         load_v(1, 0)
         load_v(1, 1)
+        load_qk(3)
+        load_qk(4)
         nc.vector.memset(key_row[:].rearrange("p j c -> p (j c)").bitcast(U32), 0)
         nc.vector.memset(t_row[:, 0:TAIL], NEVER)
         make_identity(nc, ident[:])
@@ -415,8 +417,8 @@ def tile_multiscaleretention_pb_kernel(tc, q_rot, k_rot, v, times, out):
         quantise_v(0, 1)
         done = 4
         for s in range(PAIRS + 1):
-            if s + 3 < PAIRS:
-                load_qk(s + 3)
+            if s + 5 < PAIRS:
+                load_qk(s + 5)
             g = s // HEADS + 2
             if g * HEADS < PAIRS:
                 load_v(g, s % HEADS)

@@ -20,7 +20,9 @@ QP = 32
 QUARTERS = 4
 PAIRS = H * B // 2
 SETS = B // 2
-HEADS = 2
+V_SIZES = [2, 2, 4, 4, 4]
+V_FIRST = [sum(V_SIZES[:g]) for g in range(len(V_SIZES))]
+V_MOST = max(V_SIZES)
 TAIL = 32
 GAP = P - QP
 STRIDE = P + GAP
@@ -28,16 +30,9 @@ UNITS = 6
 UNIT_COLS = [P, P, P, P, P, 2 * TAIL]
 UNIT_AT = [0, P, 2 * P, 3 * P, 4 * P, 5 * P]
 COLS = 5 * P + 2 * TAIL
-SLOT_G1, SLOT_G2, SLOT_G3, SLOT_G0 = 0, 1, 2, 3
-UNIT_PARTS = [
-    ((1, SLOT_G1), (1, SLOT_G1)),
-    ((2, SLOT_G2), (0, SLOT_G0)),
-    ((0, SLOT_G0), (2, SLOT_G2)),
-    ((3, SLOT_G3), None),
-    (None, (3, SLOT_G3)),
-]
-V_BYTES = HEADS * DH * 5
-V_CODES = HEADS * DH * 4
+UNIT_PARTS = [(1, 1), (2, 0), (0, 2), (3, None), (None, 3)]
+V_CODE = DH * 4
+V_BOTH = DH * 5
 NEVER = -(2.0**16)
 STEEP = 2.0**40
 LOG_GAMMA = [math.log(1.0 - 2.0 ** (-5 - h)) for h in range(H)]
@@ -54,8 +49,9 @@ def tile_multiscaleretention_pb_kernel(tc, q_rot, k_rot, v, times, out):
         loads = stack.enter_context(tc.tile_pool(name="loads", bufs=6))
         decays = stack.enter_context(tc.tile_pool(name="decays", bufs=3))
         weighed = stack.enter_context(tc.tile_pool(name="weighed", bufs=2))
-        values = stack.enter_context(tc.tile_pool(name="values", bufs=2))
+        values = stack.enter_context(tc.tile_pool(name="values", bufs=3))
         results = stack.enter_context(tc.tile_pool(name="results", bufs=3))
+        v_loads = stack.enter_context(tc.tile_pool(name="v_loads", bufs=3))
         turn_psum = stack.enter_context(tc.psum_pool(name="turn_psum", bufs=1))
         score_psum = stack.enter_context(tc.psum_pool(name="score_psum", bufs=4))
         out_psum = stack.enter_context(tc.psum_pool(name="out_psum", bufs=1))
@@ -85,12 +81,12 @@ def tile_multiscaleretention_pb_kernel(tc, q_rot, k_rot, v, times, out):
         v_parts = [
             [
                 [
-                    const.tile([P, V_BYTES], U8, name="v_part%d_%d_%d" % (r, w, a), align_bytes=64)
+                    const.tile([P, V_MOST * V_BOTH], U8, name="v_part%d_%d_%d" % (r, w, a), align_bytes=64)
                     for a in range(QUARTERS)
                 ]
                 for w in range(2)
             ]
-            for r in range(3)
+            for r in range(2)
         ]
 
         def load_qk(s):
@@ -105,40 +101,37 @@ def tile_multiscaleretention_pb_kernel(tc, q_rot, k_rot, v, times, out):
             )
 
         def load_v(g, which):
-            h, b = head_of(g * HEADS), first_b(g * HEADS) + which
-            v_sb[g, which] = loads.tile([P, HEADS, T, DH], BF16, name="v_sb%d" % which)
-            flat = v_sb[g, which][:].rearrange("p h t d -> p h (t d)")
-            rows = v[h : h + HEADS, b].rearrange("h (p t) d -> p h (t d)", t=T)
+            h, b, n = head_of(V_FIRST[g]), first_b(V_FIRST[g]) + which, V_SIZES[g]
+            v_sb[g, which] = v_loads.tile([P, V_MOST, T, DH], BF16, name="v_sb%d" % which)
+            flat = v_sb[g, which][:, 0:n].rearrange("p h t d -> p h (t d)")
+            rows = v[h : h + n, b].rearrange("h (p t) d -> p h (t d)", t=T)
             if which == 1:
                 nc.sync.dma_start(out=flat, in_=rows)
             else:
                 for c in range(QUARTERS):
                     at = (QUARTERS - 1 - c) * QP
-                    nc.sync.dma_start(
-                        out=flat[at : at + QP], in_=rows[c * QP : (c + 1) * QP]
-                    )
+                    nc.sync.dma_start(out=flat[at : at + QP], in_=rows[c * QP : (c + 1) * QP])
 
-        def regroup_v(g, which):
-            v_grouped[g, which] = values.tile([P, HEADS, DH, T], BF16, name="v_grouped", align_bytes=64)
+        def regroup_v(g, which, e):
+            if e == 0:
+                v_grouped[g, which] = values.tile([P, V_MOST, DH, T], BF16, name="v_grouped", align_bytes=64)
+            dst = v_grouped[g, which][:, e]
+            src = v_sb[g, which][:, e].rearrange("p t d -> p d t")
             if g == 0:
-                nc.vector.tensor_copy(
-                    out=v_grouped[g, which][:], in_=v_sb[g, which][:].rearrange("p h t d -> p h d t")
-                )
-                return
-            for e in range(HEADS):
+                nc.vector.tensor_copy(out=dst, in_=src)
+            else:
                 nc.gpsimd.tensor_scalar(
-                    out=v_grouped[g, which][:, e],
-                    in0=v_sb[g, which][:, e].rearrange("p t d -> p d t"),
-                    scalar1=1.0, scalar2=0.0, op0=ALU.mult, op1=ALU.add,
+                    out=dst, in0=src, scalar1=1.0, scalar2=0.0, op0=ALU.mult, op1=ALU.add
                 )
 
         def quantise_v(g, which):
-            parts = v_parts[g % 3][which]
+            n = V_SIZES[g]
+            parts = v_parts[g % 2][which]
             full = parts[QUARTERS - 1]
             nc.vector.quantize_mx(
-                out=full[:, 0:V_CODES].bitcast(FP8X4),
-                scales=full[:, V_CODES:V_BYTES],
-                in_=v_grouped[g, which][:].rearrange("p h d t -> p (h d t)"),
+                out=full[:, 0 : n * V_CODE].bitcast(FP8X4),
+                scales=full[:, n * V_CODE : n * V_BOTH],
+                in_=v_grouped[g, which][:, 0:n].rearrange("p h d t -> p (h d t)"),
             )
             for a in range(QUARTERS - 1):
                 live = (a + 1) * QP
@@ -146,7 +139,10 @@ def tile_multiscaleretention_pb_kernel(tc, q_rot, k_rot, v, times, out):
                     dst, src = slice(0, live), slice(P - live, P)
                 else:
                     dst, src = slice(P - live, P), slice(0, live)
-                nc.sync.dma_start(out=parts[a][dst, :].bitcast(I32), in_=full[src, :].bitcast(I32))
+                nc.sync.dma_start(
+                    out=parts[a][dst, 0 : n * V_BOTH].bitcast(I32),
+                    in_=full[src, 0 : n * V_BOTH].bitcast(I32),
+                )
 
         def turn(s):
             k_bank = turn_psum.tile([P, 2 * T, P], BF16, name="k_bank")
@@ -166,8 +162,8 @@ def tile_multiscaleretention_pb_kernel(tc, q_rot, k_rot, v, times, out):
                 in_=q_bank[:].rearrange("d (w a) p -> d w (a p)", w=2),
             )
 
-        def query_cols(slot):
-            return slice(0, P) if slot == SLOT_G0 else slice((slot + 1) * P, (slot + 2) * P)
+        def query_cols(a):
+            return slice(a * P, (a + 1) * P)
 
         def key_window(wide, w, t, a):
             flat = wide[:].rearrange("p j c -> p (j c)")
@@ -180,12 +176,12 @@ def tile_multiscaleretention_pb_kernel(tc, q_rot, k_rot, v, times, out):
             keys = k_t[s % 3]
             for t in range(T):
                 if u < 5:
-                    parts = [(w, part) for w, part in enumerate(UNIT_PARTS[u]) if part is not None]
-                    for n, (w, (a, slot)) in enumerate(parts):
+                    parts = [(w, a) for w, a in enumerate(UNIT_PARTS[u]) if a is not None]
+                    for n, (w, a) in enumerate(parts):
                         nc.tensor.matmul(
                             out=bank[:, t, :],
                             lhsT=key_window(keys, w, t, a),
-                            rhs=q_t[s % 3][:, w, query_cols(slot)],
+                            rhs=q_t[s % 3][:, w, query_cols(a)],
                             start=n == 0,
                             stop=n == len(parts) - 1,
                         )
@@ -239,50 +235,47 @@ def tile_multiscaleretention_pb_kernel(tc, q_rot, k_rot, v, times, out):
 
         def product(s):
             h, b0 = head_of(s), first_b(s)
-            e = s % HEADS
-            out_sb = results.tile([P, 2, 4, DH], F32, name="out_sb")
+            g = max(i for i in range(len(V_SIZES)) if V_FIRST[i] <= s)
+            n, e = V_SIZES[g], s - V_FIRST[g]
+            out_sb = results.tile([P, 2 * QUARTERS, DH], F32, name="out_sb")
+            rows = out[h, b0 : b0 + 2].rearrange("b l d -> (b l) d")
+            body = rows[P - TAIL : 2 * L - TAIL, :].rearrange("(a p) d -> p a d", p=P)
             for w in range(2):
-                parts = v_parts[(s // HEADS) % 3][w]
-                bank = out_psum.tile([P, 4, DH], F32, name="out_bank%d" % w)
+                bank = out_psum.tile([P, QUARTERS, DH], F32, name="out_bank%d" % w)
 
-                def multiply(slot, codes, scales, a, start, stop):
+                def multiply(slot, codes, scales, owner, a, start, stop):
+                    values_of = v_parts[g % 2][owner][a]
                     nc.tensor.matmul_mx(
                         out=bank[:, slot, :],
                         lhsT=codes.bitcast(FP8X4),
                         lhsT_scale=scales,
-                        rhs=parts[a][:, e * 4 * DH : (e + 1) * 4 * DH].bitcast(FP8X4),
-                        rhs_scale=parts[a][:, V_CODES + e * DH : V_CODES + (e + 1) * DH],
+                        rhs=values_of[:, e * V_CODE : (e + 1) * V_CODE].bitcast(FP8X4),
+                        rhs_scale=values_of[:, n * V_CODE + e * DH : n * V_CODE + (e + 1) * DH],
                         start=start,
                         stop=stop,
                     )
 
                 for u in range(5):
-                    part = UNIT_PARTS[u][w]
-                    if part is None:
+                    a = UNIT_PARTS[u][w]
+                    if a is None:
                         continue
-                    a, slot = part
                     cols = slice(u * P, (u + 1) * P)
-                    has_tail = slot == SLOT_G0
-                    multiply(slot, ret_codes[s][:, cols], ret_scales[s][:, cols], a, True, not has_tail)
-                    if has_tail:
-                        tail = slice(w * P, (w + 1) * P)
+                    multiply(a, ret_codes[s][:, cols], ret_scales[s][:, cols], w, a, True, a > 0)
+                    if a == 0:
+                        other = 1 - w
+                        tail = slice(other * P, (other + 1) * P)
                         multiply(
-                            slot, tail_codes[s % 2][:, tail], tail_scales[s % 2][:, tail],
-                            QUARTERS - 1, False, True,
+                            a, tail_codes[s % 2][:, tail], tail_scales[s % 2][:, tail],
+                            other, QUARTERS - 1, False, True,
                         )
-                nc.scalar.copy(out=out_sb[:, w, :, :], in_=bank[:])
-                nc.sync.dma_start(
-                    out=out[h, b0 + w, P - TAIL : L - TAIL, :].rearrange("(a p) d -> p a d", p=P),
-                    in_=out_sb[:, w, 0:3, :],
-                )
-            nc.sync.dma_start(
-                out=out[h, b0 : b0 + 2, 0 : P - TAIL, :].rearrange("b p d -> p b d"),
-                in_=out_sb[TAIL:P, :, 3, :],
-            )
-            nc.sync.dma_start(
-                out=out[h, b0 : b0 + 2, L - TAIL : L, :].rearrange("b p d -> p b d"),
-                in_=out_sb[0:TAIL, :, 3, :],
-            )
+                nc.scalar.copy(out=out_sb[:, w * QUARTERS : (w + 1) * QUARTERS, :], in_=bank[:])
+                if s == PAIRS - 1:
+                    lo, hi = (0, 3) if w == 0 else (3, 7)
+                    nc.sync.dma_start(out=body[:, lo:hi, :], in_=out_sb[:, lo + 1 : hi + 1, :])
+            if s < PAIRS - 1:
+                nc.sync.dma_start(out=body, in_=out_sb[:, 1 : 2 * QUARTERS, :])
+            nc.sync.dma_start(out=rows[0 : P - TAIL, :], in_=out_sb[TAIL:P, 0, :])
+            nc.sync.dma_start(out=rows[2 * L - TAIL : 2 * L, :], in_=out_sb[0:TAIL, 0, :])
 
         nc.vector.memset(t_row[:].bitcast(U32), 0)
         nc.sync.dma_start(out=t_row[0:P:32, TAIL : TAIL + L], in_=times)
@@ -337,18 +330,18 @@ def tile_multiscaleretention_pb_kernel(tc, q_rot, k_rot, v, times, out):
             bank_a = out_psum.tile([P, T, P], F32, name="out_bank0")
             bank_b = out_psum.tile([P, T, P], F32, name="out_bank1")
             for u in range(5):
-                parts = [(w, part) for w, part in enumerate(UNIT_PARTS[u]) if part is not None]
+                parts = [(w, a) for w, a in enumerate(UNIT_PARTS[u]) if a is not None]
                 dst = bank_a[:, u, :] if u < 4 else bank_b[:, 0, :]
-                for n, (w, (a, slot)) in enumerate(parts):
+                for n, (w, a) in enumerate(parts):
                     nc.tensor.matmul(
                         out=dst,
                         lhsT=ones_window(2 * g + w, w, a),
-                        rhs=t_row[:, query_cols(slot)],
+                        rhs=t_row[:, query_cols(a)],
                         start=n == 0,
                         stop=n == len(parts) - 1,
                     )
                 for t in range(T):
-                    for n, (w, (a, slot)) in enumerate(parts):
+                    for n, (w, a) in enumerate(parts):
                         b = 2 * g + w
                         nc.tensor.matmul(
                             out=bank_b[:, 2, u * T + t : u * T + t + 1],
@@ -404,24 +397,35 @@ def tile_multiscaleretention_pb_kernel(tc, q_rot, k_rot, v, times, out):
         turn(1)
         decay_of(1, [0, 1, 2])
         decay_of(1, [3, 4, 5])
-        for r in range(3):
+        def zero_v_parts(r, lo, hi):
             for w in range(2):
                 for a in range(QUARTERS):
-                    nc.gpsimd.memset(v_parts[r][w][a][:].bitcast(I32), 0)
-            if r < 2:
-                nc.gpsimd.memset(tail_codes[r][:], 0)
-                nc.gpsimd.memset(tail_scales[r][:].bitcast(I32), 0)
-        regroup_v(0, 0)
-        regroup_v(0, 1)
+                    nc.gpsimd.memset(v_parts[r][w][a][:].bitcast(I32)[:, lo:hi], 0)
+
+        small, most = V_SIZES[0] * V_BOTH // 4, V_MOST * V_BOTH // 4
+        zero_v_parts(0, 0, small)
+        for r in range(2):
+            nc.gpsimd.memset(tail_codes[r][:], 0)
+            nc.gpsimd.memset(tail_scales[r][:].bitcast(I32), 0)
+        zero_v_parts(1, 0, small)
+        for w in range(2):
+            for e in range(V_SIZES[0]):
+                regroup_v(0, w, e)
         quantise_v(0, 0)
         quantise_v(0, 1)
         done = 4
         for s in range(PAIRS + 1):
             if s + 5 < PAIRS:
                 load_qk(s + 5)
-            g = s // HEADS + 2
-            if g * HEADS < PAIRS:
-                load_v(g, s % HEADS)
+            g = max(i for i in range(len(V_SIZES)) if V_FIRST[i] <= s)
+            ahead = s - V_FIRST[g]
+            if g + 2 < len(V_SIZES) and ahead < 2:
+                load_v(g + 2, ahead)
+            pieces = []
+            if g + 1 < len(V_SIZES):
+                n = V_SIZES[g + 1]
+                share = 2 * n // V_SIZES[g]
+                pieces = [divmod(i, n) for i in range(ahead * share, (ahead + 1) * share)]
             if s + 2 < PAIRS:
                 turn(s + 2)
             for u in range(UNITS):
@@ -439,12 +443,13 @@ def tile_multiscaleretention_pb_kernel(tc, q_rot, k_rot, v, times, out):
                 if u == 1 and s >= 1:
                     quantise_rest(s - 1)
                     product(s - 1)
-                g = s // HEADS + 1
-                if g * HEADS < PAIRS:
-                    if u == 3:
-                        regroup_v(g, s % HEADS)
-                    if u == 5:
-                        quantise_v(g, s % HEADS)
+                for w, e in pieces:
+                    if u == 0:
+                        regroup_v(g + 1, w, e)
+                    if u == 5 and e == n - 1:
+                        quantise_v(g + 1, w)
             if s < UNITS:
                 subtract(1, s, nc.gpsimd)
                 make_delta(1, s)
+            if s in (0, 2):
+                zero_v_parts(s // 2, small, most)

@@ -20,9 +20,7 @@ QP = 32
 QUARTERS = 4
 PAIRS = H * B // 2
 SETS = B // 2
-V_SIZES = [2, 2, 4, 4, 4]
-V_FIRST = [sum(V_SIZES[:g]) for g in range(len(V_SIZES))]
-V_MOST = max(V_SIZES)
+HEADS = 2
 TAIL = 32
 GAP = P - QP
 STRIDE = P + GAP
@@ -31,8 +29,8 @@ UNIT_COLS = [P, P, P, P, P, 2 * TAIL]
 UNIT_AT = [0, P, 2 * P, 3 * P, 4 * P, 5 * P]
 COLS = 5 * P + 2 * TAIL
 UNIT_PARTS = [(1, 1), (2, 0), (0, 2), (3, None), (None, 3)]
-V_CODE = DH * 4
-V_BOTH = DH * 5
+V_CODES = HEADS * DH * 4
+V_BYTES = HEADS * DH * 5
 NEVER = -(2.0**16)
 STEEP = 2.0**40
 LOG_GAMMA = [math.log(1.0 - 2.0 ** (-5 - h)) for h in range(H)]
@@ -57,6 +55,7 @@ def tile_multiscaleretention_pb_kernel(tc, q_rot, k_rot, v, times, out):
         out_psum = stack.enter_context(tc.psum_pool(name="out_psum", bufs=1))
 
         q_sb, k_sb, v_sb, v_grouped = {}, {}, {}, {}
+        k_banks = {}
         scores, decay, ret_bf, ret_codes, ret_scales = {}, {}, {}, {}, {}
 
         def head_of(s):
@@ -66,12 +65,12 @@ def tile_multiscaleretention_pb_kernel(tc, q_rot, k_rot, v, times, out):
             return 2 * (s // H)
 
         ident = const.tile([P, P], BF16, name="ident")
-        swapped = const.tile([P, P], BF16, name="swapped")
+        chosen = const.tile([P, 2, STRIDE], BF16, name="chosen")
         t_row = const.tile([P, TAIL + L], BF16, name="t_row")
-        key_row = const.tile([P, 2 * T, STRIDE], BF16, name="key_row")
+        key_times = const.tile([P, 2, SETS, T], BF16, name="key_times")
         ones = [const.tile([P, GAP + P + GAP], BF16, name="ones%d" % b) for b in range(B)]
         q_time = [const.tile([P, COLS], F32, name="q_time%d" % g) for g in range(SETS)]
-        k_time = [const.tile([P, 5 * T], F32, name="k_time%d" % g) for g in range(SETS)]
+        k_time = const.tile([P, 5, SETS, T], F32, name="k_time")
         diff = const.tile([P, COLS, T], F32, name="diff")
         delta = [const.tile([P, COLS, T], F32, name="delta%d" % g) for g in range(SETS)]
         k_t = [const.tile([P, 2 * T, STRIDE], BF16, name="k_t%d" % r) for r in range(3)]
@@ -81,7 +80,7 @@ def tile_multiscaleretention_pb_kernel(tc, q_rot, k_rot, v, times, out):
         v_parts = [
             [
                 [
-                    const.tile([P, V_MOST * V_BOTH], U8, name="v_part%d_%d_%d" % (r, w, a), align_bytes=64)
+                    const.tile([P, V_BYTES], U8, name="v_part%d_%d_%d" % (r, w, a), align_bytes=64)
                     for a in range(QUARTERS)
                 ]
                 for w in range(2)
@@ -101,10 +100,10 @@ def tile_multiscaleretention_pb_kernel(tc, q_rot, k_rot, v, times, out):
             )
 
         def load_v(g, which):
-            h, b, n = head_of(V_FIRST[g]), first_b(V_FIRST[g]) + which, V_SIZES[g]
-            v_sb[g, which] = v_loads.tile([P, V_MOST, T, DH], BF16, name="v_sb%d" % which)
-            flat = v_sb[g, which][:, 0:n].rearrange("p h t d -> p h (t d)")
-            rows = v[h : h + n, b].rearrange("h (p t) d -> p h (t d)", t=T)
+            h, b = head_of(g * HEADS), first_b(g * HEADS) + which
+            v_sb[g, which] = v_loads.tile([P, HEADS, T, DH], BF16, name="v_sb%d" % which)
+            flat = v_sb[g, which][:].rearrange("p h t d -> p h (t d)")
+            rows = v[h : h + HEADS, b].rearrange("h (p t) d -> p h (t d)", t=T)
             if which == 1:
                 nc.sync.dma_start(out=flat, in_=rows)
             else:
@@ -114,7 +113,7 @@ def tile_multiscaleretention_pb_kernel(tc, q_rot, k_rot, v, times, out):
 
         def regroup_v(g, which, e):
             if e == 0:
-                v_grouped[g, which] = values.tile([P, V_MOST, DH, T], BF16, name="v_grouped", align_bytes=64)
+                v_grouped[g, which] = values.tile([P, HEADS, DH, T], BF16, name="v_grouped", align_bytes=64)
             dst = v_grouped[g, which][:, e]
             src = v_sb[g, which][:, e].rearrange("p t d -> p d t")
             if g == 0:
@@ -125,13 +124,12 @@ def tile_multiscaleretention_pb_kernel(tc, q_rot, k_rot, v, times, out):
                 )
 
         def quantise_v(g, which):
-            n = V_SIZES[g]
             parts = v_parts[g % 2][which]
             full = parts[QUARTERS - 1]
             nc.vector.quantize_mx(
-                out=full[:, 0 : n * V_CODE].bitcast(FP8X4),
-                scales=full[:, n * V_CODE : n * V_BOTH],
-                in_=v_grouped[g, which][:, 0:n].rearrange("p h d t -> p (h d t)"),
+                out=full[:, 0:V_CODES].bitcast(FP8X4),
+                scales=full[:, V_CODES:V_BYTES],
+                in_=v_grouped[g, which][:].rearrange("p h d t -> p (h d t)"),
             )
             for a in range(QUARTERS - 1):
                 live = (a + 1) * QP
@@ -139,10 +137,7 @@ def tile_multiscaleretention_pb_kernel(tc, q_rot, k_rot, v, times, out):
                     dst, src = slice(0, live), slice(P - live, P)
                 else:
                     dst, src = slice(P - live, P), slice(0, live)
-                nc.sync.dma_start(
-                    out=parts[a][dst, 0 : n * V_BOTH].bitcast(I32),
-                    in_=full[src, 0 : n * V_BOTH].bitcast(I32),
-                )
+                nc.sync.dma_start(out=parts[a][dst, :].bitcast(I32), in_=full[src, :].bitcast(I32))
 
         def turn(s):
             k_bank = turn_psum.tile([P, 2 * T, P], BF16, name="k_bank")
@@ -151,23 +146,26 @@ def tile_multiscaleretention_pb_kernel(tc, q_rot, k_rot, v, times, out):
                     nc.tensor.transpose(
                         out=k_bank[:, w * T + t, :],
                         in_=k_sb[s][:, w, t * DH : (t + 1) * DH],
-                        identity=swapped[:] if w == 0 else ident[:],
+                        identity=chosen[:, w, 0:P],
                     )
             q_bank = turn_psum.tile([P, 2 * T, P], BF16, name="q_bank")
             for a in range(2 * T):
                 nc.tensor.transpose(out=q_bank[:, a, :], in_=q_sb[s][:, a, :], identity=ident[:])
-            nc.scalar.copy(out=k_t[s % 3][:, :, 0:P], in_=k_bank[:])
+            k_banks[s] = k_bank
             nc.scalar.copy(
                 out=q_t[s % 3][:, :, TAIL : TAIL + L],
                 in_=q_bank[:].rearrange("d (w a) p -> d w (a p)", w=2),
             )
 
+        def empty_k_bank(s):
+            nc.vector.tensor_copy(out=k_t[s % 3][:, :, 0:P], in_=k_banks[s][:])
+
         def query_cols(a):
             return slice(a * P, (a + 1) * P)
 
-        def key_window(wide, w, t, a):
+        def key_window(wide, j, w, a):
             flat = wide[:].rearrange("p j c -> p (j c)")
-            at = (w * T + t) * STRIDE + (1 - 2 * w) * (QUARTERS - 1 - a) * QP
+            at = j * STRIDE + (1 - 2 * w) * (QUARTERS - 1 - a) * QP
             return flat[:, at : at + P]
 
         def score(s, u):
@@ -180,7 +178,7 @@ def tile_multiscaleretention_pb_kernel(tc, q_rot, k_rot, v, times, out):
                     for n, (w, a) in enumerate(parts):
                         nc.tensor.matmul(
                             out=bank[:, t, :],
-                            lhsT=key_window(keys, w, t, a),
+                            lhsT=key_window(keys, w * T + t, w, a),
                             rhs=q_t[s % 3][:, w, query_cols(a)],
                             start=n == 0,
                             stop=n == len(parts) - 1,
@@ -189,7 +187,7 @@ def tile_multiscaleretention_pb_kernel(tc, q_rot, k_rot, v, times, out):
                     for w in range(2):
                         nc.tensor.matmul(
                             out=bank[:, t, w * TAIL : (w + 1) * TAIL],
-                            lhsT=key_window(keys, w, t, QUARTERS - 1),
+                            lhsT=key_window(keys, w * T + t, w, QUARTERS - 1),
                             rhs=q_t[s % 3][:, w, L : L + TAIL],
                             start=True,
                             stop=True,
@@ -222,21 +220,21 @@ def tile_multiscaleretention_pb_kernel(tc, q_rot, k_rot, v, times, out):
                 in_=ret_bf[s][:, at : at + width, :].rearrange("p i t -> p (i t)"),
             )
 
-        def quantise_main(s):
-            ret_codes[s] = weighed.tile([P, 5 * P], U32, name="ret_codes", align_bytes=64)
-            ret_scales[s] = weighed.tile([P, 5 * P], U8, name="ret_scales", align_bytes=64)
-            quantise(s, 0, 4 * P, ret_codes[s][:, 0 : 4 * P], ret_scales[s][:, 0 : 4 * P])
+        def quantise_units(s, u, n):
+            if u == 0:
+                ret_codes[s] = weighed.tile([P, 5 * P], U32, name="ret_codes", align_bytes=64)
+                ret_scales[s] = weighed.tile([P, 5 * P], U8, name="ret_scales", align_bytes=64)
+            cols = slice(u * P, (u + n) * P)
+            quantise(s, u * P, n * P, ret_codes[s][:, cols], ret_scales[s][:, cols])
 
-        def quantise_rest(s):
-            quantise(s, 4 * P, P, ret_codes[s][:, 4 * P : 5 * P], ret_scales[s][:, 4 * P : 5 * P])
+        def quantise_tails(s):
             for w in range(2):
                 cols = slice(w * P, w * P + TAIL)
                 quantise(s, 5 * P + w * TAIL, TAIL, tail_codes[s % 2][:, cols], tail_scales[s % 2][:, cols])
 
         def product(s):
             h, b0 = head_of(s), first_b(s)
-            g = max(i for i in range(len(V_SIZES)) if V_FIRST[i] <= s)
-            n, e = V_SIZES[g], s - V_FIRST[g]
+            g, e = divmod(s, HEADS)
             out_sb = results.tile([P, 2 * QUARTERS, DH], F32, name="out_sb")
             rows = out[h, b0 : b0 + 2].rearrange("b l d -> (b l) d")
             body = rows[P - TAIL : 2 * L - TAIL, :].rearrange("(a p) d -> p a d", p=P)
@@ -249,16 +247,14 @@ def tile_multiscaleretention_pb_kernel(tc, q_rot, k_rot, v, times, out):
                         out=bank[:, slot, :],
                         lhsT=codes.bitcast(FP8X4),
                         lhsT_scale=scales,
-                        rhs=values_of[:, e * V_CODE : (e + 1) * V_CODE].bitcast(FP8X4),
-                        rhs_scale=values_of[:, n * V_CODE + e * DH : n * V_CODE + (e + 1) * DH],
+                        rhs=values_of[:, e * 4 * DH : (e + 1) * 4 * DH].bitcast(FP8X4),
+                        rhs_scale=values_of[:, V_CODES + e * DH : V_CODES + (e + 1) * DH],
                         start=start,
                         stop=stop,
                     )
 
-                for u in range(5):
-                    a = UNIT_PARTS[u][w]
-                    if a is None:
-                        continue
+                for a in (1, 2, 3, 0):
+                    u = [parts[w] for parts in UNIT_PARTS].index(a)
                     cols = slice(u * P, (u + 1) * P)
                     multiply(a, ret_codes[s][:, cols], ret_scales[s][:, cols], w, a, True, a > 0)
                     if a == 0:
@@ -268,7 +264,8 @@ def tile_multiscaleretention_pb_kernel(tc, q_rot, k_rot, v, times, out):
                             a, tail_codes[s % 2][:, tail], tail_scales[s % 2][:, tail],
                             other, QUARTERS - 1, False, True,
                         )
-                nc.scalar.copy(out=out_sb[:, w * QUARTERS : (w + 1) * QUARTERS, :], in_=bank[:])
+                copy = nc.vector.tensor_copy if w == 1 and s == PAIRS - 1 else nc.scalar.copy
+                copy(out=out_sb[:, w * QUARTERS : (w + 1) * QUARTERS, :], in_=bank[:])
                 if s == PAIRS - 1:
                     lo, hi = (0, 3) if w == 0 else (3, 7)
                     nc.sync.dma_start(out=body[:, lo:hi, :], in_=out_sb[:, lo + 1 : hi + 1, :])
@@ -288,7 +285,7 @@ def tile_multiscaleretention_pb_kernel(tc, q_rot, k_rot, v, times, out):
         load_v(1, 1)
         load_qk(3)
         load_qk(4)
-        nc.vector.memset(key_row[:].rearrange("p j c -> p (j c)").bitcast(U32), 0)
+        nc.vector.memset(chosen[:].rearrange("p j c -> p (j c)").bitcast(U32), 0)
         nc.vector.memset(t_row[:, 0:TAIL], NEVER)
         make_identity(nc, ident[:])
         for b in range(B):
@@ -297,8 +294,9 @@ def tile_multiscaleretention_pb_kernel(tc, q_rot, k_rot, v, times, out):
         for c in range(QUARTERS):
             far = QUARTERS - 1 - c
             nc.vector.tensor_copy(
-                out=swapped[:, c * QP : (c + 1) * QP], in_=ident[:, far * QP : (far + 1) * QP]
+                out=chosen[:, 0, c * QP : (c + 1) * QP], in_=ident[:, far * QP : (far + 1) * QP]
             )
+        nc.vector.tensor_copy(out=chosen[:, 1, 0:P], in_=ident[:])
         for r in range(3):
             nc.gpsimd.memset(
                 k_t[r][:].rearrange("p j c -> p (j c)").bitcast(U32).rearrange("p (j c) -> p j c", j=2 * T)[
@@ -311,22 +309,39 @@ def tile_multiscaleretention_pb_kernel(tc, q_rot, k_rot, v, times, out):
             for w in range(2):
                 nc.gpsimd.memset(q_t[r][:, w, 0:TAIL].bitcast(U32), 0)
 
-        times_only = t_row[:, TAIL : TAIL + L]
-        for c in range(QUARTERS):
-            far = QUARTERS - 1 - c
-            nc.vector.tensor_copy(
-                out=key_row[:, 0:T, far * QP : (far + 1) * QP],
-                in_=times_only[:, c * P : (c + 1) * P].rearrange("p (r t) -> p t r", t=T),
-            )
-        nc.vector.tensor_copy(
-            out=key_row[:, T : 2 * T, 0:P], in_=times_only.rearrange("p (m t) -> p t m", t=T)
-        )
-
         def ones_window(b, w, a):
             at = GAP + (1 - 2 * w) * (QUARTERS - 1 - a) * QP
             return ones[b][:, at : at + P]
 
-        def time_banks(g):
+        def key_side():
+            bank = score_psum.tile([P, T, P], F32, name="score_bank")
+            groups = t_row[:, TAIL : TAIL + L].rearrange("p (m t) -> p t m", t=T)
+            for t in range(T):
+                nc.tensor.matmul(
+                    out=bank[:, 0, t * B : (t + 1) * B],
+                    lhsT=groups[:, t, :],
+                    rhs=ident[:, 0:P:32],
+                    start=True,
+                    stop=True,
+                )
+            nc.vector.tensor_copy(
+                out=key_times[:],
+                in_=bank[:, 0, 0 : T * B].rearrange("p (t g w) -> p w g t", t=T, g=SETS),
+            )
+            bank = score_psum.tile([P, T, P], F32, name="score_bank")
+            for u in range(5):
+                parts = [(w, a) for w, a in enumerate(UNIT_PARTS[u]) if a is not None]
+                for n, (w, a) in enumerate(parts):
+                    nc.tensor.matmul(
+                        out=bank[:, 0, u * SETS * T : (u + 1) * SETS * T],
+                        lhsT=key_window(chosen, w, w, a),
+                        rhs=key_times[:, w].rearrange("p g t -> p (g t)"),
+                        start=n == 0,
+                        stop=n == len(parts) - 1,
+                    )
+            return bank
+
+        def query_side(g):
             bank_a = out_psum.tile([P, T, P], F32, name="out_bank0")
             bank_b = out_psum.tile([P, T, P], F32, name="out_bank1")
             for u in range(5):
@@ -340,16 +355,6 @@ def tile_multiscaleretention_pb_kernel(tc, q_rot, k_rot, v, times, out):
                         start=n == 0,
                         stop=n == len(parts) - 1,
                     )
-                for t in range(T):
-                    for n, (w, a) in enumerate(parts):
-                        b = 2 * g + w
-                        nc.tensor.matmul(
-                            out=bank_b[:, 2, u * T + t : u * T + t + 1],
-                            lhsT=key_window(key_row, w, t, a),
-                            rhs=ident[:, 32 * b : 32 * b + 1],
-                            start=n == 0,
-                            stop=n == len(parts) - 1,
-                        )
             for w in range(2):
                 nc.tensor.matmul(
                     out=bank_b[:, 1, w * TAIL : (w + 1) * TAIL],
@@ -358,7 +363,9 @@ def tile_multiscaleretention_pb_kernel(tc, q_rot, k_rot, v, times, out):
                     start=True,
                     stop=True,
                 )
-            nc.vector.tensor_copy(out=k_time[g][:], in_=bank_b[:, 2, 0 : 5 * T])
+            return bank_a, bank_b
+
+        def keep_query_side(g, bank_a, bank_b):
             nc.vector.tensor_copy(
                 out=q_time[g][:, 0 : 4 * P], in_=bank_a[:].rearrange("p u i -> p (u i)")
             )
@@ -374,7 +381,7 @@ def tile_multiscaleretention_pb_kernel(tc, q_rot, k_rot, v, times, out):
                 engine.tensor_tensor(
                     out=diff[:, at : at + width, :],
                     in0=q_time[g][:, at : at + width].unsqueeze(2).to_broadcast([P, width, T]),
-                    in1=k_time[g][:, k_unit * T : (k_unit + 1) * T].unsqueeze(1).to_broadcast([P, width, T]),
+                    in1=k_time[:, k_unit, g].unsqueeze(1).to_broadcast([P, width, T]),
                     op=ALU.subtract,
                 )
 
@@ -386,30 +393,34 @@ def tile_multiscaleretention_pb_kernel(tc, q_rot, k_rot, v, times, out):
             )
 
         order = [(s, u) for s in range(PAIRS) for u in range(UNITS)]
-        time_banks(0)
+        k_time_bank = key_side()
+        first_sides = query_side(0)
+        nc.vector.tensor_copy(
+            out=k_time[:].rearrange("p u g t -> p (u g t)"), in_=k_time_bank[:, 0, 0 : 5 * SETS * T]
+        )
+        keep_query_side(0, *first_sides)
         turn(0)
         for u in range(UNITS):
             subtract(0, u, nc.vector if u < 3 else nc.gpsimd)
             make_delta(0, u)
+            if u == 0:
+                empty_k_bank(0)
             decay_of(0, [u])
             if u < 4:
                 score(*order[u])
         turn(1)
+        empty_k_bank(1)
         decay_of(1, [0, 1, 2])
         decay_of(1, [3, 4, 5])
-        def zero_v_parts(r, lo, hi):
-            for w in range(2):
-                for a in range(QUARTERS):
-                    nc.gpsimd.memset(v_parts[r][w][a][:].bitcast(I32)[:, lo:hi], 0)
 
-        small, most = V_SIZES[0] * V_BOTH // 4, V_MOST * V_BOTH // 4
-        zero_v_parts(0, 0, small)
         for r in range(2):
+            for w in range(2):
+                for part in v_parts[r][w]:
+                    nc.gpsimd.memset(part[:].bitcast(I32), 0)
             nc.gpsimd.memset(tail_codes[r][:], 0)
             nc.gpsimd.memset(tail_scales[r][:].bitcast(I32), 0)
-        zero_v_parts(1, 0, small)
         for w in range(2):
-            for e in range(V_SIZES[0]):
+            for e in range(HEADS):
                 regroup_v(0, w, e)
         quantise_v(0, 0)
         quantise_v(0, 1)
@@ -417,17 +428,14 @@ def tile_multiscaleretention_pb_kernel(tc, q_rot, k_rot, v, times, out):
         for s in range(PAIRS + 1):
             if s + 5 < PAIRS:
                 load_qk(s + 5)
-            g = max(i for i in range(len(V_SIZES)) if V_FIRST[i] <= s)
-            ahead = s - V_FIRST[g]
-            if g + 2 < len(V_SIZES) and ahead < 2:
-                load_v(g + 2, ahead)
-            pieces = []
-            if g + 1 < len(V_SIZES):
-                n = V_SIZES[g + 1]
-                share = 2 * n // V_SIZES[g]
-                pieces = [divmod(i, n) for i in range(ahead * share, (ahead + 1) * share)]
+            g, which = divmod(s, HEADS)
+            if (g + 2) * HEADS < PAIRS:
+                load_v(g + 2, which)
+            next_v = (g + 1) * HEADS < PAIRS
             if s + 2 < PAIRS:
                 turn(s + 2)
+            if 1 <= s <= UNITS:
+                subtract(1, s - 1, nc.gpsimd)
             for u in range(UNITS):
                 if s < PAIRS:
                     weigh(s, u)
@@ -436,20 +444,25 @@ def tile_multiscaleretention_pb_kernel(tc, q_rot, k_rot, v, times, out):
                         done += 1
                 if s + 2 < PAIRS and u % 2 == 0:
                     decay_of(s + 2, [u, u + 1])
+                if u == 2 and s + 2 < PAIRS:
+                    empty_k_bank(s + 2)
+                if u == 3 and 1 <= s <= UNITS:
+                    make_delta(1, s - 1)
                 if u == 1 and s == 0:
-                    time_banks(1)
-                if u == 0 and s >= 1:
-                    quantise_main(s - 1)
+                    second_sides = query_side(1)
+                if u == 3 and s == 0:
+                    keep_query_side(1, *second_sides)
+                if u == 0 and 1 <= s < PAIRS:
+                    quantise_units(s - 1, 0, 4)
+                if u == 1 and 1 <= s < PAIRS:
+                    quantise_units(s - 1, 4, 1)
                 if u == 1 and s >= 1:
-                    quantise_rest(s - 1)
+                    quantise_tails(s - 1)
                     product(s - 1)
-                for w, e in pieces:
-                    if u == 0:
-                        regroup_v(g + 1, w, e)
-                    if u == 5 and e == n - 1:
-                        quantise_v(g + 1, w)
-            if s < UNITS:
-                subtract(1, s, nc.gpsimd)
-                make_delta(1, s)
-            if s in (0, 2):
-                zero_v_parts(s // 2, small, most)
+                if s == PAIRS - 1 and u in (2, 4, 5):
+                    quantise_units(s, *{2: (0, 2), 4: (2, 2), 5: (4, 1)}[u])
+                if next_v and u == 0:
+                    for e in range(HEADS):
+                        regroup_v(g + 1, which, e)
+                if next_v and u == 5:
+                    quantise_v(g + 1, which)

@@ -55,7 +55,6 @@ def tile_multiscaleretention_pb_kernel(tc, q_rot, k_rot, v, times, out):
         out_psum = stack.enter_context(tc.psum_pool(name="out_psum", bufs=1))
 
         q_sb, k_sb, v_sb, v_grouped = {}, {}, {}, {}
-        k_banks = {}
         scores, decay, ret_bf, ret_codes, ret_scales = {}, {}, {}, {}, {}
 
         def head_of(s):
@@ -139,7 +138,7 @@ def tile_multiscaleretention_pb_kernel(tc, q_rot, k_rot, v, times, out):
                     dst, src = slice(P - live, P), slice(0, live)
                 nc.sync.dma_start(out=parts[a][dst, :].bitcast(I32), in_=full[src, :].bitcast(I32))
 
-        def turn(s):
+        def turn_k(s):
             k_bank = turn_psum.tile([P, 2 * T, P], BF16, name="k_bank")
             for w in range(2):
                 for t in range(T):
@@ -148,17 +147,16 @@ def tile_multiscaleretention_pb_kernel(tc, q_rot, k_rot, v, times, out):
                         in_=k_sb[s][:, w, t * DH : (t + 1) * DH],
                         identity=chosen[:, w, 0:P],
                     )
+            nc.scalar.copy(out=k_t[s % 3][:, :, 0:P], in_=k_bank[:])
+
+        def turn_q(s):
             q_bank = turn_psum.tile([P, 2 * T, P], BF16, name="q_bank")
             for a in range(2 * T):
                 nc.tensor.transpose(out=q_bank[:, a, :], in_=q_sb[s][:, a, :], identity=ident[:])
-            k_banks[s] = k_bank
             nc.scalar.copy(
                 out=q_t[s % 3][:, :, TAIL : TAIL + L],
                 in_=q_bank[:].rearrange("d (w a) p -> d w (a p)", w=2),
             )
-
-        def empty_k_bank(s):
-            nc.vector.tensor_copy(out=k_t[s % 3][:, :, 0:P], in_=k_banks[s][:])
 
         def query_cols(a):
             return slice(a * P, (a + 1) * P)
@@ -399,17 +397,16 @@ def tile_multiscaleretention_pb_kernel(tc, q_rot, k_rot, v, times, out):
             out=k_time[:].rearrange("p u g t -> p (u g t)"), in_=k_time_bank[:, 0, 0 : 5 * SETS * T]
         )
         keep_query_side(0, *first_sides)
-        turn(0)
+        turn_k(0)
+        turn_q(0)
         for u in range(UNITS):
             subtract(0, u, nc.vector if u < 3 else nc.gpsimd)
             make_delta(0, u)
-            if u == 0:
-                empty_k_bank(0)
             decay_of(0, [u])
             if u < 4:
                 score(*order[u])
-        turn(1)
-        empty_k_bank(1)
+        turn_k(1)
+        turn_q(1)
         decay_of(1, [0, 1, 2])
         decay_of(1, [3, 4, 5])
 
@@ -432,8 +429,6 @@ def tile_multiscaleretention_pb_kernel(tc, q_rot, k_rot, v, times, out):
             if (g + 2) * HEADS < PAIRS:
                 load_v(g + 2, which)
             next_v = (g + 1) * HEADS < PAIRS
-            if s + 2 < PAIRS:
-                turn(s + 2)
             if 1 <= s <= UNITS:
                 subtract(1, s - 1, nc.gpsimd)
             for u in range(UNITS):
@@ -444,10 +439,12 @@ def tile_multiscaleretention_pb_kernel(tc, q_rot, k_rot, v, times, out):
                         done += 1
                 if s + 2 < PAIRS and u % 2 == 0:
                     decay_of(s + 2, [u, u + 1])
-                if u == 2 and s + 2 < PAIRS:
-                    empty_k_bank(s + 2)
                 if u == 3 and 1 <= s <= UNITS:
                     make_delta(1, s - 1)
+                if u == 2 and s + 2 < PAIRS:
+                    turn_k(s + 2)
+                if u == 4 and s + 2 < PAIRS:
+                    turn_q(s + 2)
                 if u == 1 and s == 0:
                     second_sides = query_side(1)
                 if u == 3 and s == 0:

import math
from contextlib import ExitStack

import concourse.mybir as mybir
from concourse.masks import make_identity

F32 = mybir.dt.float32
BF16 = mybir.dt.bfloat16
U32 = mybir.dt.uint32
I32 = mybir.dt.int32
U8 = mybir.dt.uint8
FP8X4 = mybir.dt.float8_e4m3fn_x4
ALU = mybir.AluOpType
ACT = mybir.ActivationFunctionType

H, B, L, DH = 8, 4, 512, 128
P = 128
T = 4
QP = 32
QUARTERS = 4
PAIRS = H * B // 2
SETS = B // 2
HEADS = 2
TAIL = 32
GAP = P - QP
STRIDE = P + GAP
UNITS = 6
UNIT_COLS = [P, P, P, P, P, 2 * TAIL]
UNIT_AT = [0, P, 2 * P, 3 * P, 4 * P, 5 * P]
COLS = 5 * P + 2 * TAIL
UNIT_PARTS = [(1, 1), (2, 0), (0, 2), (3, None), (None, 3)]
V_CODES = HEADS * DH * 4
V_BYTES = HEADS * DH * 5
NEVER = -(2.0**16)
STEEP = 2.0**40
LOG_GAMMA = [math.log(1.0 - 2.0 ** (-5 - h)) for h in range(H)]

FLOPS = 2 * (2 * H * B * L * L * DH)


def tile_multiscaleretention_pb_kernel(tc, q_rot, k_rot, v, times, out):
    nc = tc.nc

    with ExitStack() as stack:
        stack.enter_context(tc.manual_schedule())
        const = stack.enter_context(tc.tile_pool(name="const", bufs=1))
        loads = stack.enter_context(tc.tile_pool(name="loads", bufs=6))
        decays = stack.enter_context(tc.tile_pool(name="decays", bufs=3))
        weighed = stack.enter_context(tc.tile_pool(name="weighed", bufs=2))
        values = stack.enter_context(tc.tile_pool(name="values", bufs=3))
        results = stack.enter_context(tc.tile_pool(name="results", bufs=3))
        v_loads = stack.enter_context(tc.tile_pool(name="v_loads", bufs=3))
        turn_psum = stack.enter_context(tc.psum_pool(name="turn_psum", bufs=1))
        score_psum = stack.enter_context(tc.psum_pool(name="score_psum", bufs=4))
        out_psum = stack.enter_context(tc.psum_pool(name="out_psum", bufs=1))

        q_sb, k_sb, v_sb, v_grouped = {}, {}, {}, {}
        scores, decay, ret_bf, ret_codes, ret_scales = {}, {}, {}, {}, {}

        def head_of(s):
            return s % H

        def first_b(s):
            return 2 * (s // H)

        ident = const.tile([P, P], BF16, name="ident")
        chosen = const.tile([P, 2, STRIDE], BF16, name="chosen")
        t_row = const.tile([P, TAIL + L], BF16, name="t_row")
        key_times = const.tile([P, 2, SETS, T], BF16, name="key_times")
        ones = [const.tile([P, GAP + P + GAP], BF16, name="ones%d" % b) for b in range(B)]
        q_time = [const.tile([P, COLS], F32, name="q_time%d" % g) for g in range(SETS)]
        k_time = const.tile([P, 5, SETS, T], F32, name="k_time")
        diff = const.tile([P, COLS, T], F32, name="diff")
        delta = [const.tile([P, COLS, T], F32, name="delta%d" % g) for g in range(SETS)]
        k_t = [const.tile([P, 2 * T, STRIDE], BF16, name="k_t%d" % r) for r in range(3)]
        q_t = [const.tile([P, 2, TAIL + L], BF16, name="q_t%d" % r) for r in range(3)]
        tail_codes = [const.tile([P, 2 * P], U32, name="tail_codes%d" % r, align_bytes=64) for r in range(2)]
        tail_scales = [const.tile([P, 2 * P], U8, name="tail_scales%d" % r, align_bytes=64) for r in range(2)]
        v_parts = [
            [
                [
                    const.tile([P, V_BYTES], U8, name="v_part%d_%d_%d" % (r, w, a), align_bytes=64)
                    for a in range(QUARTERS)
                ]
                for w in range(2)
            ]
            for r in range(2)
        ]

        def load_qk(s):
            h, b0 = head_of(s), first_b(s)
            k_sb[s] = loads.tile([P, 2, T * DH], BF16, name="k_sb")
            q_sb[s] = loads.tile([P, 2 * T, DH], BF16, name="q_sb")
            nc.sync.dma_start(
                out=k_sb[s][:], in_=k_rot[h, b0 : b0 + 2].rearrange("b (p t) d -> p b (t d)", t=T)
            )
            nc.sync.dma_start(
                out=q_sb[s][:], in_=q_rot[h, b0 : b0 + 2].rearrange("b l d -> (b l) d").rearrange("(a p) d -> p a d", p=P)
            )

        def load_v(g, which):
            h, b = head_of(g * HEADS), first_b(g * HEADS) + which
            v_sb[g, which] = v_loads.tile([P, HEADS, T, DH], BF16, name="v_sb%d" % which)
            flat = v_sb[g, which][:].rearrange("p h t d -> p h (t d)")
            rows = v[h : h + HEADS, b].rearrange("h (p t) d -> p h (t d)", t=T)
            if which == 1:
                nc.sync.dma_start(out=flat, in_=rows)
            else:
                for c in range(QUARTERS):
                    at = (QUARTERS - 1 - c) * QP
                    nc.sync.dma_start(out=flat[at : at + QP], in_=rows[c * QP : (c + 1) * QP])

        def regroup_v(g, which, e):
            if e == 0:
                v_grouped[g, which] = values.tile([P, HEADS, DH, T], BF16, name="v_grouped", align_bytes=64)
            dst = v_grouped[g, which][:, e]
            src = v_sb[g, which][:, e].rearrange("p t d -> p d t")
            if g == 0:
                nc.vector.tensor_copy(out=dst, in_=src)
            else:
                nc.gpsimd.tensor_scalar(
                    out=dst, in0=src, scalar1=1.0, scalar2=0.0, op0=ALU.mult, op1=ALU.add
                )

        def quantise_v(g, which):
            parts = v_parts[g % 2][which]
            full = parts[QUARTERS - 1]
            nc.vector.quantize_mx(
                out=full[:, 0:V_CODES].bitcast(FP8X4),
                scales=full[:, V_CODES:V_BYTES],
                in_=v_grouped[g, which][:].rearrange("p h d t -> p (h d t)"),
            )
            for a in range(QUARTERS - 1):
                live = (a + 1) * QP
                if which == 0:
                    dst, src = slice(0, live), slice(P - live, P)
                else:
                    dst, src = slice(P - live, P), slice(0, live)
                nc.sync.dma_start(out=parts[a][dst, :].bitcast(I32), in_=full[src, :].bitcast(I32))

        def turn_k(s):
            k_bank = turn_psum.tile([P, 2 * T, P], BF16, name="k_bank")
            for w in range(2):
                for t in range(T):
                    nc.tensor.transpose(
                        out=k_bank[:, w * T + t, :],
                        in_=k_sb[s][:, w, t * DH : (t + 1) * DH],
                        identity=chosen[:, w, 0:P],
                    )
            nc.scalar.copy(out=k_t[s % 3][:, :, 0:P], in_=k_bank[:])

        def turn_q(s):
            q_bank = turn_psum.tile([P, 2 * T, P], BF16, name="q_bank")
            for a in range(2 * T):
                nc.tensor.transpose(out=q_bank[:, a, :], in_=q_sb[s][:, a, :], identity=ident[:])
            nc.scalar.copy(
                out=q_t[s % 3][:, :, TAIL : TAIL + L],
                in_=q_bank[:].rearrange("d (w a) p -> d w (a p)", w=2),
            )

        def query_cols(a):
            return slice(a * P, (a + 1) * P)

        def key_window(wide, j, w, a):
            flat = wide[:].rearrange("p j c -> p (j c)")
            at = j * STRIDE + (1 - 2 * w) * (QUARTERS - 1 - a) * QP
            return flat[:, at : at + P]

        def score(s, u):
            bank = score_psum.tile([P, T, P], F32, name="score_bank")
            scores[s, u] = bank
            keys = k_t[s % 3]
            for t in range(T):
                if u < 5:
                    parts = [(w, a) for w, a in enumerate(UNIT_PARTS[u]) if a is not None]
                    for n, (w, a) in enumerate(parts):
                        nc.tensor.matmul(
                            out=bank[:, t, :],
                            lhsT=key_window(keys, w * T + t, w, a),
                            rhs=q_t[s % 3][:, w, query_cols(a)],
                            start=n == 0,
                            stop=n == len(parts) - 1,
                        )
                else:
                    for w in range(2):
                        nc.tensor.matmul(
                            out=bank[:, t, w * TAIL : (w + 1) * TAIL],
                            lhsT=key_window(keys, w * T + t, w, QUARTERS - 1),
                            rhs=q_t[s % 3][:, w, L : L + TAIL],
                            start=True,
                            stop=True,
                        )

        def decay_of(s, units):
            if s not in decay:
                decay[s] = decays.tile([P, COLS, T], F32, name="decay")
            cols = slice(UNIT_AT[units[0]], UNIT_AT[units[-1]] + UNIT_COLS[units[-1]])
            nc.scalar.activation(
                out=decay[s][:, cols, :], in_=delta[s // H][:, cols, :], func=ACT.Exp,
                scale=LOG_GAMMA[head_of(s)],
            )

        def weigh(s, u):
            if u == 0:
                ret_bf[s] = weighed.tile([P, COLS, T], BF16, name="ret_bf", align_bytes=64)
            cols = slice(UNIT_AT[u], UNIT_AT[u] + UNIT_COLS[u])
            nc.vector.tensor_tensor(
                out=ret_bf[s][:, cols, :],
                in0=scores[s, u][:, :, 0 : UNIT_COLS[u]].rearrange("p t i -> p i t"),
                in1=decay[s][:, cols, :],
                op=ALU.mult,
            )

        def quantise(s, at, width, codes, scales):
            nc.vector.quantize_mx(
                out=codes.bitcast(FP8X4),
                scales=scales,
                in_=ret_bf[s][:, at : at + width, :].rearrange("p i t -> p (i t)"),
            )

        def quantise_units(s, u, n):
            if u == 0:
                ret_codes[s] = weighed.tile([P, 5 * P], U32, name="ret_codes", align_bytes=64)
                ret_scales[s] = weighed.tile([P, 5 * P], U8, name="ret_scales", align_bytes=64)
            cols = slice(u * P, (u + n) * P)
            quantise(s, u * P, n * P, ret_codes[s][:, cols], ret_scales[s][:, cols])

        def quantise_tails(s):
            for w in range(2):
                cols = slice(w * P, w * P + TAIL)
                quantise(s, 5 * P + w * TAIL, TAIL, tail_codes[s % 2][:, cols], tail_scales[s % 2][:, cols])

        def product(s):
            h, b0 = head_of(s), first_b(s)
            g, e = divmod(s, HEADS)
            out_sb = results.tile([P, 2 * QUARTERS, DH], F32, name="out_sb")
            rows = out[h, b0 : b0 + 2].rearrange("b l d -> (b l) d")
            body = rows[P - TAIL : 2 * L - TAIL, :].rearrange("(a p) d -> p a d", p=P)
            for w in range(2):
                bank = out_psum.tile([P, QUARTERS, DH], F32, name="out_bank%d" % w)

                def multiply(slot, codes, scales, owner, a, start, stop):
                    values_of = v_parts[g % 2][owner][a]
                    nc.tensor.matmul_mx(
                        out=bank[:, slot, :],
                        lhsT=codes.bitcast(FP8X4),
                        lhsT_scale=scales,
                        rhs=values_of[:, e * 4 * DH : (e + 1) * 4 * DH].bitcast(FP8X4),
                        rhs_scale=values_of[:, V_CODES + e * DH : V_CODES + (e + 1) * DH],
                        start=start,
                        stop=stop,
                    )

                for a in (1, 2, 3, 0):
                    u = [parts[w] for parts in UNIT_PARTS].index(a)
                    cols = slice(u * P, (u + 1) * P)
                    multiply(a, ret_codes[s][:, cols], ret_scales[s][:, cols], w, a, True, a > 0)
                    if a == 0:
                        other = 1 - w
                        tail = slice(other * P, (other + 1) * P)
                        multiply(
                            a, tail_codes[s % 2][:, tail], tail_scales[s % 2][:, tail],
                            other, QUARTERS - 1, False, True,
                        )
                copy = nc.vector.tensor_copy if w == 1 and s == PAIRS - 1 else nc.scalar.copy
                copy(out=out_sb[:, w * QUARTERS : (w + 1) * QUARTERS, :], in_=bank[:])
                if s == PAIRS - 1:
                    lo, hi = (0, 3) if w == 0 else (3, 7)
                    nc.sync.dma_start(out=body[:, lo:hi, :], in_=out_sb[:, lo + 1 : hi + 1, :])
            if s < PAIRS - 1:
                nc.sync.dma_start(out=body, in_=out_sb[:, 1 : 2 * QUARTERS, :])
            nc.sync.dma_start(out=rows[0 : P - TAIL, :], in_=out_sb[TAIL:P, 0, :])
            nc.sync.dma_start(out=rows[2 * L - TAIL : 2 * L, :], in_=out_sb[0:TAIL, 0, :])

        nc.vector.memset(t_row[:].bitcast(U32), 0)
        nc.sync.dma_start(out=t_row[0:P:32, TAIL : TAIL + L], in_=times)
        load_qk(0)
        load_qk(1)
        load_v(0, 0)
        load_v(0, 1)
        load_qk(2)
        load_v(1, 0)
        load_v(1, 1)
        load_qk(3)
        load_qk(4)
        nc.vector.memset(chosen[:].rearrange("p j c -> p (j c)").bitcast(U32), 0)
        nc.vector.memset(t_row[:, 0:TAIL], NEVER)
        make_identity(nc, ident[:])
        for b in range(B):
            nc.gpsimd.memset(ones[b][:].bitcast(U32), 0)
            nc.gpsimd.memset(ones[b][32 * b : 32 * b + 1, GAP : GAP + P], 1.0)
        for c in range(QUARTERS):
            far = QUARTERS - 1 - c
            nc.vector.tensor_copy(
                out=chosen[:, 0, c * QP : (c + 1) * QP], in_=ident[:, far * QP : (far + 1) * QP]
            )
        nc.vector.tensor_copy(out=chosen[:, 1, 0:P], in_=ident[:])
        for r in range(3):
            nc.gpsimd.memset(
                k_t[r][:].rearrange("p j c -> p (j c)").bitcast(U32).rearrange("p (j c) -> p j c", j=2 * T)[
                    :, :, P // 2 : STRIDE // 2
                ],
                0,
            )

        for r in range(3):
            for w in range(2):
                nc.gpsimd.memset(q_t[r][:, w, 0:TAIL].bitcast(U32), 0)

        def ones_window(b, w, a):
            at = GAP + (1 - 2 * w) * (QUARTERS - 1 - a) * QP
            return ones[b][:, at : at + P]

        def key_side():
            bank = score_psum.tile([P, T, P], F32, name="score_bank")
            groups = t_row[:, TAIL : TAIL + L].rearrange("p (m t) -> p t m", t=T)
            for t in range(T):
                nc.tensor.matmul(
                    out=bank[:, 0, t * B : (t + 1) * B],
                    lhsT=groups[:, t, :],
                    rhs=ident[:, 0:P:32],
                    start=True,
                    stop=True,
                )
            nc.vector.tensor_copy(
                out=key_times[:],
                in_=bank[:, 0, 0 : T * B].rearrange("p (t g w) -> p w g t", t=T, g=SETS),
            )
            bank = score_psum.tile([P, T, P], F32, name="score_bank")
            for u in range(5):
                parts = [(w, a) for w, a in enumerate(UNIT_PARTS[u]) if a is not None]
                for n, (w, a) in enumerate(parts):
                    nc.tensor.matmul(
                        out=bank[:, 0, u * SETS * T : (u + 1) * SETS * T],
                        lhsT=key_window(chosen, w, w, a),
                        rhs=key_times[:, w].rearrange("p g t -> p (g t)"),
                        start=n == 0,
                        stop=n == len(parts) - 1,
                    )
            return bank

        def query_side(g):
            bank_a = out_psum.tile([P, T, P], F32, name="out_bank0")
            bank_b = out_psum.tile([P, T, P], F32, name="out_bank1")
            for u in range(5):
                parts = [(w, a) for w, a in enumerate(UNIT_PARTS[u]) if a is not None]
                dst = bank_a[:, u, :] if u < 4 else bank_b[:, 0, :]
                for n, (w, a) in enumerate(parts):
                    nc.tensor.matmul(
                        out=dst,
                        lhsT=ones_window(2 * g + w, w, a),
                        rhs=t_row[:, query_cols(a)],
                        start=n == 0,
                        stop=n == len(parts) - 1,
                    )
            for w in range(2):
                nc.tensor.matmul(
                    out=bank_b[:, 1, w * TAIL : (w + 1) * TAIL],
                    lhsT=ones_window(2 * g + w, w, QUARTERS - 1),
                    rhs=t_row[:, L : L + TAIL],
                    start=True,
                    stop=True,
                )
            return bank_a, bank_b

        def keep_query_side(g, bank_a, bank_b):
            nc.vector.tensor_copy(
                out=q_time[g][:, 0 : 4 * P], in_=bank_a[:].rearrange("p u i -> p (u i)")
            )
            nc.scalar.copy(
                out=q_time[g][:, 4 * P : COLS],
                in_=bank_b[:].rearrange("p u i -> p (u i)")[:, 0 : P + 2 * TAIL],
            )

        def subtract(g, u, engine):
            at = UNIT_AT[u]
            pieces = [(u, at, P)] if u < 5 else [(3, at, TAIL), (4, at + TAIL, TAIL)]
            for k_unit, at, width in pieces:
                engine.tensor_tensor(
                    out=diff[:, at : at + width, :],
                    in0=q_time[g][:, at : at + width].unsqueeze(2).to_broadcast([P, width, T]),
                    in1=k_time[:, k_unit, g].unsqueeze(1).to_broadcast([P, width, T]),
                    op=ALU.subtract,
                )

        def make_delta(g, u):
            cols = slice(UNIT_AT[u], UNIT_AT[u] + UNIT_COLS[u])
            nc.vector.scalar_tensor_tensor(
                out=delta[g][:, cols, :], in0=diff[:, cols, :], scalar=-STEEP, in1=diff[:, cols, :],
                op0=ALU.mult, op1=ALU.max,
            )

        order = [(s, u) for s in range(PAIRS) for u in range(UNITS)]
        k_time_bank = key_side()
        first_sides = query_side(0)
        nc.vector.tensor_copy(
            out=k_time[:].rearrange("p u g t -> p (u g t)"), in_=k_time_bank[:, 0, 0 : 5 * SETS * T]
        )
        keep_query_side(0, *first_sides)
        turn_k(0)
        turn_q(0)
        for u in range(UNITS):
            subtract(0, u, nc.vector if u < 3 else nc.gpsimd)
            make_delta(0, u)
            decay_of(0, [u])
            if u < 4:
                score(*order[u])
        turn_k(1)
        turn_q(1)
        decay_of(1, [0, 1, 2])
        decay_of(1, [3, 4, 5])

        for r in range(2):
            for w in range(2):
                for part in v_parts[r][w]:
                    nc.gpsimd.memset(part[:].bitcast(I32), 0)
            nc.gpsimd.memset(tail_codes[r][:], 0)
            nc.gpsimd.memset(tail_scales[r][:].bitcast(I32), 0)
        for w in range(2):
            for e in range(HEADS):
                regroup_v(0, w, e)
        quantise_v(0, 0)
        quantise_v(0, 1)
        done = 4
        for s in range(PAIRS + 1):
            if s + 5 < PAIRS:
                load_qk(s + 5)
            g, which = divmod(s, HEADS)
            if (g + 2) * HEADS < PAIRS:
                load_v(g + 2, which)
            next_v = (g + 1) * HEADS < PAIRS
            if 1 <= s <= UNITS:
                subtract(1, s - 1, nc.gpsimd)
            for u in range(UNITS):
                if s < PAIRS:
                    weigh(s, u)
                    if done < len(order):
                        score(*order[done])
                        done += 1
                if s + 2 < PAIRS and u % 2 == 0:
                    decay_of(s + 2, [u, u + 1])
                if u == 3 and 1 <= s <= UNITS:
                    make_delta(1, s - 1)
                if u == 2 and s + 2 < PAIRS:
                    turn_k(s + 2)
                if u == 4 and s + 2 < PAIRS:
                    turn_q(s + 2)
                if u == 1 and s == 0:
                    second_sides = query_side(1)
                if u == 3 and s == 0:
                    keep_query_side(1, *second_sides)
                if u == 0 and 1 <= s < PAIRS:
                    quantise_units(s - 1, 0, 4)
                if u == 1 and 1 <= s < PAIRS:
                    quantise_units(s - 1, 4, 1)
                if u == 1 and s >= 1:
                    quantise_tails(s - 1)
                    product(s - 1)
                if s == PAIRS - 1 and u in (2, 4, 5):
                    quantise_units(s, *{2: (0, 2), 4: (2, 2), 5: (4, 1)}[u])
                if next_v and u == 0:
                    for e in range(HEADS):
                        regroup_v(g + 1, which, e)
                if next_v and u == 5:
                    quantise_v(g + 1, which)
